import numpy as np
import ml_dtypes


def mxq(x, axis, fmt="e4m3"):
    dtype, down = {"e4m3": (ml_dtypes.float8_e4m3fn, 7), "e5m2": (ml_dtypes.float8_e5m2, 14)}[fmt]
    v = np.moveaxis(np.asarray(x, np.float32).astype(ml_dtypes.bfloat16).astype(np.float64), axis, -1)
    blocks = v.reshape(v.shape[:-1] + (-1, 32))
    amax = np.abs(blocks).max(-1, keepdims=True)
    byte = np.maximum(np.where(amax > 0, np.frexp(amax)[1] - 1 + 127, 0) - down, 1)
    scale = np.exp2(byte - 127.0)
    codes = (blocks / scale).astype(np.float32).astype(dtype).astype(np.float64)
    return np.moveaxis((codes * scale).reshape(v.shape), -1, axis)


WIDE = False


def mx_kscale(k):
    if not WIDE:
        return np.ones(k)
    levels = np.array([10, -10, 5, -5, 0])
    a = np.random.permutation(np.resize(levels, k // 512 * 4)).reshape(k // 512, 4)
    idx = np.arange(k)
    return np.exp2(a[idx // 512, idx % 128 // 32])


BF16 = ml_dtypes.bfloat16


def bf(x):
    return np.asarray(x, np.float32).astype(BF16)


def f64(x):
    return np.asarray(x).astype(np.float64)


B, H, S, D, C = 8, 4, 512, 128, 512


def decay_mask():
    gamma = 1.0 - 2.0 ** (-5.0 - np.arange(H))
    i = np.arange(S)[:, None]
    j = np.arange(S)[None, :]
    tri = i >= j
    expo = np.where(tri, i - j, 0)
    return np.where(tri[None], gamma[:, None, None] ** expo[None], 0.0)[None]


def setup_inputs():
    t = mx_kscale(S)
    t = t / t.max()
    omask = bf(decay_mask())
    L = f64(omask).sum(-1, keepdims=True)
    return {"q_scaled": bf(np.random.standard_normal((B, H, S, D)) / L),
            "k": bf(np.random.standard_normal((B, H, S, D)) * t[:, None]),
            "v": bf(np.random.standard_normal((B, H, S, D)) / t[:, None]),
            "omask": omask}


def reference(q_scaled, k, v, omask):
    qs, kk, om = f64(q_scaled), f64(k), f64(omask)
    vq = mxq(f64(v), 2, "e4m3")
    rows = []
    for r in range(S // C):
        a, e = r * C, (r + 1) * C
        sc = (qs[:, :, a:e] @ kk[:, :, :e].transpose(0, 1, 3, 2)) * om[0][None, :, a:e, :e]
        p = np.maximum(np.abs(sc.sum(-1)), 1.0)[..., None]
        rows.append((mxq(sc, 3, "e4m3") @ vq[:, :, :e]) / p)
    return np.concatenate(rows, axis=2)

@@ -1,0 +1,179 @@
+from contextlib import ExitStack
+
+import concourse.bass as bass
+import concourse.mybir as mybir
+import concourse.tile as tile
+from concourse.masks import make_identity
+
+BF16 = mybir.dt.bfloat16
+F32 = mybir.dt.float32
+U32 = mybir.dt.uint32
+U8 = mybir.dt.uint8
+FP8X4 = mybir.dt.float8_e4m3fn_x4
+ALU = mybir.AluOpType
+ACT = mybir.ActivationFunctionType
+
+B, H, S, D = 8, 4, 512, 128
+P = 128
+NH = B * H
+FLOPS = NH * 2 * (2 * S * S * D)
+
+LAG_T = 2
+LAG_X = 1
+LAG_Q = 2
+LAG_O = 4
+
+
+def tile_parallelretention_fast3_pa_t_kernel(tc, q_scaled, k, v, omask, out):
+    nc = tc.nc
+    with ExitStack() as ctx:
+        const = ctx.enter_context(tc.tile_pool(name="const", bufs=1))
+        res = ctx.enter_context(tc.tile_pool(name="res", bufs=1))
+        work = ctx.enter_context(tc.tile_pool(name="work", bufs=3))
+        psum = ctx.enter_context(tc.psum_pool(name="psum", bufs=1))
+
+        ident_b = const.tile([P, P], BF16, name="ident_b")
+        make_identity(nc, ident_b[:])
+        ident_f = const.tile([P, P], F32, name="ident_f")
+        make_identity(nc, ident_f[:])
+
+        q_sb, k_sb, v_sb, om_sb, vcodes, vscales = [], [], [], [], [], []
+        for g in range(B):
+            q_sb.append(res.tile([P, H, S], BF16, name="q_sb%d" % g))
+            k_sb.append(res.tile([P, H * 4, D], BF16, name="k_sb%d" % g))
+            v_sb.append(res.tile([P, H * 2, 2 * D], BF16, name="v_sb%d" % g))
+            vcodes.append(res.tile([P, H * D], U32, name="vcodes%d" % g, align_bytes=64))
+            vscales.append(res.tile([P, H * D], U8, name="vscales%d" % g, align_bytes=64))
+        for h in range(H):
+            om_sb.append(res.tile([P, 4 * S], BF16, name="om_sb%d" % h))
+
+        for h in range(H):
+            nc.sync.dma_start(out=k_sb[0][:, 4 * h:4 * h + 4, :],
+                              in_=k[0, h].rearrange("(m r) d -> r m d", r=P))
+            nc.sync.dma_start(out=q_sb[0][:, h, :],
+                              in_=q_scaled[0, h].rearrange("(p c) d -> p (c d)", c=4))
+            nc.sync.dma_start(out=om_sb[h][:],
+                              in_=omask[0, h].rearrange("(p c) j -> p (c j)", c=4))
+        nc.sync.dma_start(out=v_sb[0][:],
+                          in_=v[0].rearrange("h (u p e) d -> p (h u) (e d)", u=2, e=2))
+        for g in range(1, B):
+            nc.sync.dma_start(out=k_sb[g][:],
+                              in_=k[g].rearrange("h (m r) d -> r (h m) d", r=P))
+            nc.sync.dma_start(out=q_sb[g][:],
+                              in_=q_scaled[g].rearrange("h (p c) d -> p h (c d)", c=4))
+            nc.sync.dma_start(out=v_sb[g][:],
+                              in_=v[g].rearrange("h (u p e) d -> p (h u) (e d)", u=2, e=2))
+
+        qkT, sc_bf, grouped, codes, scales, rs, rp, vg = {}, {}, {}, {}, {}, {}, {}, {}
+        qk_ps, x_ps = {}, {}
+
+        def t_qk(n, part):
+            g, h = divmod(n, H)
+            if part == 0:
+                qk_ps[n] = psum.tile([P, 2 * S], BF16, name="qk_ps", bufs=2)
+            for idx in (2 * part, 2 * part + 1):
+                if idx < 4:
+                    src = k_sb[g][:, 4 * h + idx, :]
+                else:
+                    src = q_sb[g][:, h, (idx - 4) * D:(idx - 3) * D]
+                nc.tensor.transpose(qk_ps[n][:, idx * P:(idx + 1) * P], src, ident_b[:])
+            if part == 3:
+                qkT[n] = work.tile([P, 2 * S], BF16, name="qkT")
+                nc.scalar.copy(out=qkT[n][:], in_=qk_ps[n][:])
+
+        def score(n, c):
+            g, h = divmod(n, H)
+            if c == 0:
+                sc_bf[n] = work.tile([P, 4 * S], BF16, name="sc_bf")
+                if h == 0:
+                    rs[g] = work.tile([P, 4 * H], F32, name="rs")
+            s_ps = psum.tile([P, S], F32, name="s_ps", bufs=3)
+            nc.tensor.matmul(out=s_ps[:], lhsT=qkT[n][:, S + c * P:S + (c + 1) * P],
+                             rhs=qkT[n][:, 0:S], start=True, stop=True)
+            nc.vector.scalar_tensor_tensor(
+                out=sc_bf[n][:, c * S:(c + 1) * S], in0=s_ps[:], scalar=1.0,
+                in1=om_sb[h][:, c * S:(c + 1) * S], op0=ALU.mult, op1=ALU.mult,
+                accum_out=rs[g][:, 4 * h + c:4 * h + c + 1])
+
+        def t_sc(n, c):
+            cp, c2 = divmod(c, 2)
+            if c == 0:
+                grouped[n] = work.tile([P, 4 * S], BF16, name="grouped", align_bytes=64)
+            if c2 == 0:
+                x_ps[n] = psum.tile([P, S], F32, name="x_ps", bufs=2)
+            words = sc_bf[n][:].bitcast(F32)
+            for u in range(2):
+                nc.tensor.transpose(x_ps[n][:, u * 256 + c2 * P:u * 256 + (c2 + 1) * P],
+                                    words[:, c * 256 + u * P:c * 256 + (u + 1) * P], ident_f[:])
+            if c2 == 1:
+                gw = grouped[n][:].bitcast(F32)
+                nc.scalar.copy(
+                    out=gw[:, cp * S:(cp + 1) * S].rearrange("p (x u) -> p x u", u=2),
+                    in_=x_ps[n][:].rearrange("p (u x) -> p x u", u=2))
+
+        def quant(n):
+            codes[n] = work.tile([P, S], U32, name="codes", bufs=4, align_bytes=64)
+            scales[n] = work.tile([P, S], U8, name="scales", bufs=4, align_bytes=64)
+            nc.vector.quantize_mx(out=codes[n][:].bitcast(FP8X4), scales=scales[n][:],
+                                  in_=grouped[n][:])
+
+        def v_regroup(n):
+            g, h = divmod(n, H)
+            if h == 0:
+                vg[g] = work.tile([P, H, D, 4], BF16, name="vg", bufs=2, align_bytes=64)
+            src = v_sb[g][:, 2 * h:2 * h + 2, :].rearrange("p u (e d) -> p d (u e)", e=2)
+            nc.gpsimd.tensor_scalar(out=vg[g][:, h, :, :], in0=src, scalar1=1.0, scalar2=0.0,
+                                    op0=ALU.mult, op1=ALU.add)
+
+        def v_quant(g):
+            nc.vector.quantize_mx(out=vcodes[g][:].bitcast(FP8X4), scales=vscales[g][:],
+                                  in_=vg[g][:].rearrange("p h d t -> p (h d t)"))
+
+        def p_ops(g):
+            ab = work.tile([P, 4 * H], F32, name="ab")
+            rp[g] = work.tile([P, 4 * H], F32, name="rp")
+            nc.vector.scalar_tensor_tensor(out=ab[:], in0=rs[g][:], scalar=-1.0, in1=rs[g][:],
+                                           op0=ALU.mult, op1=ALU.max)
+            nc.vector.tensor_scalar_max(out=ab[:], in0=ab[:], scalar1=1.0)
+            nc.vector.reciprocal(out=rp[g][:], in_=ab[:])
+
+        def output(n):
+            g, h = divmod(n, H)
+            o_ps = psum.tile([P, S], F32, name="o_ps", bufs=1)
+            for c in range(4):
+                cols = slice(c * P, (c + 1) * P)
+                nc.tensor.matmul_mx(out=o_ps[:, cols],
+                                    lhsT=codes[n][:, cols].bitcast(FP8X4),
+                                    lhsT_scale=scales[n][:, cols],
+                                    rhs=vcodes[g][:, h * D:(h + 1) * D].bitcast(FP8X4),
+                                    rhs_scale=vscales[g][:, h * D:(h + 1) * D],
+                                    start=True, stop=True)
+            o_sb = work.tile([P, S], F32, name="o_sb", bufs=4)
+            for c in range(4):
+                cols = slice(c * P, (c + 1) * P)
+                nc.scalar.activation(out=o_sb[:, cols], in_=o_ps[:, cols], func=ACT.Copy,
+                                     scale=rp[g][:, 4 * h + c:4 * h + c + 1])
+            nc.scalar.dma_start(out=out[g, h].rearrange("(p c) d -> p (c d)", c=4), in_=o_sb[:])
+
+        for n in range(LAG_T):
+            for part in range(4):
+                t_qk(n, part)
+            v_regroup(n)
+
+        for step in range(NH + LAG_O):
+            if 0 <= step - LAG_O < NH:
+                output(step - LAG_O)
+            for c in range(4):
+                if step < NH:
+                    score(step, c)
+                if step + LAG_T < NH:
+                    t_qk(step + LAG_T, c)
+                if 0 <= step - LAG_X < NH:
+                    t_sc(step - LAG_X, c)
+            if step + 2 < NH:
+                v_regroup(step + 2)
+            if 0 <= step - LAG_Q < NH:
+                quant(step - LAG_Q)
+            if step < NH and step % H == H - 1:
+                v_quant(step // H)
+                p_ops(step // H)

@@ -39,33 +39,45 @@ def tile_parallelretention_fast3_pa_t_kernel(tc, q_scaled, k, v, omask, out):
 
         q_sb, k_sb, v_sb, om_sb, vcodes, vscales = [], [], [], [], [], []
         for g in range(B):
-            q_sb.append(res.tile([P, H, S], BF16, name="q_sb%d" % g))
+            q_sb.append(res.tile([P, H * 4, D], BF16, name="q_sb%d" % g))
             k_sb.append(res.tile([P, H * 4, D], BF16, name="k_sb%d" % g))
             v_sb.append(res.tile([P, H * 2, 2 * D], BF16, name="v_sb%d" % g))
             vcodes.append(res.tile([P, H * D], U32, name="vcodes%d" % g, align_bytes=64))
             vscales.append(res.tile([P, H * D], U8, name="vscales%d" % g, align_bytes=64))
         for h in range(H):
-            om_sb.append(res.tile([P, 4 * S], BF16, name="om_sb%d" % h))
+            om_sb.append(res.tile([P, 4, S], BF16, name="om_sb%d" % h))
+
+        sc_tiles = []
+        for i in range(3):
+            t = res.tile([P, 4 * S], BF16, name="sc_tile%d" % i)
+            nc.vector.memset(t[:, P:2 * P], 0.0)
+            nc.vector.memset(t[:, 2 * S + 3 * P:3 * S], 0.0)
+            sc_tiles.append(t)
+        zero_f = const.tile([P, P], F32, name="zero_f")
+        nc.vector.memset(zero_f[:], 0.0)
+        x_banks = [psum.tile([P, S], F32, name="x_bank%d" % i) for i in range(2)]
+        for u in range(2):
+            nc.tensor.transpose(x_banks[0][:, 256 + u * P:256 + (u + 1) * P], zero_f[:], ident_f[:])
 
         for h in range(H):
             nc.sync.dma_start(out=k_sb[0][:, 4 * h:4 * h + 4, :],
                               in_=k[0, h].rearrange("(m r) d -> r m d", r=P))
-            nc.sync.dma_start(out=q_sb[0][:, h, :],
-                              in_=q_scaled[0, h].rearrange("(p c) d -> p (c d)", c=4))
+            nc.sync.dma_start(out=q_sb[0][:, 4 * h:4 * h + 4, :],
+                              in_=q_scaled[0, h].rearrange("(c p) d -> p c d", p=P))
             nc.sync.dma_start(out=om_sb[h][:],
-                              in_=omask[0, h].rearrange("(p c) j -> p (c j)", c=4))
+                              in_=omask[0, h].rearrange("(c p) j -> p c j", p=P))
         nc.sync.dma_start(out=v_sb[0][:],
                           in_=v[0].rearrange("h (u p e) d -> p (h u) (e d)", u=2, e=2))
         for g in range(1, B):
             nc.sync.dma_start(out=k_sb[g][:],
                               in_=k[g].rearrange("h (m r) d -> r (h m) d", r=P))
             nc.sync.dma_start(out=q_sb[g][:],
-                              in_=q_scaled[g].rearrange("h (p c) d -> p h (c d)", c=4))
+                              in_=q_scaled[g].rearrange("h (c p) d -> p (h c) d", p=P))
             nc.sync.dma_start(out=v_sb[g][:],
                               in_=v[g].rearrange("h (u p e) d -> p (h u) (e d)", u=2, e=2))
 
         qkT, sc_bf, grouped, codes, scales, rs, rp, vg = {}, {}, {}, {}, {}, {}, {}, {}
-        qk_ps, x_ps = {}, {}
+        qk_ps = {}
 
         def t_qk(n, part):
             g, h = divmod(n, H)
@@ -75,7 +87,7 @@ def tile_parallelretention_fast3_pa_t_kernel(tc, q_scaled, k, v, omask, out):
                 if idx < 4:
                     src = k_sb[g][:, 4 * h + idx, :]
                 else:
-                    src = q_sb[g][:, h, (idx - 4) * D:(idx - 3) * D]
+                    src = q_sb[g][:, 4 * h + idx - 4, :]
                 nc.tensor.transpose(qk_ps[n][:, idx * P:(idx + 1) * P], src, ident_b[:])
             if part == 3:
                 qkT[n] = work.tile([P, 2 * S], BF16, name="qkT")
@@ -84,32 +96,31 @@ def tile_parallelretention_fast3_pa_t_kernel(tc, q_scaled, k, v, omask, out):
         def score(n, c):
             g, h = divmod(n, H)
             if c == 0:
-                sc_bf[n] = work.tile([P, 4 * S], BF16, name="sc_bf")
+                sc_bf[n] = sc_tiles[n % 3]
                 if h == 0:
                     rs[g] = work.tile([P, 4 * H], F32, name="rs")
             s_ps = psum.tile([P, S], F32, name="s_ps", bufs=3)
-            nc.tensor.matmul(out=s_ps[:], lhsT=qkT[n][:, S + c * P:S + (c + 1) * P],
-                             rhs=qkT[n][:, 0:S], start=True, stop=True)
+            keys = (c + 1) * P
+            nc.tensor.matmul(out=s_ps[:, 0:keys], lhsT=qkT[n][:, S + c * P:S + (c + 1) * P],
+                             rhs=qkT[n][:, 0:keys], start=True, stop=True)
             nc.vector.scalar_tensor_tensor(
-                out=sc_bf[n][:, c * S:(c + 1) * S], in0=s_ps[:], scalar=1.0,
-                in1=om_sb[h][:, c * S:(c + 1) * S], op0=ALU.mult, op1=ALU.mult,
+                out=sc_bf[n][:, c * S:c * S + keys], in0=s_ps[:, 0:keys], scalar=1.0,
+                in1=om_sb[h][:, c, 0:keys], op0=ALU.mult, op1=ALU.mult,
                 accum_out=rs[g][:, 4 * h + c:4 * h + c + 1])
 
         def t_sc(n, c):
             cp, c2 = divmod(c, 2)
             if c == 0:
                 grouped[n] = work.tile([P, 4 * S], BF16, name="grouped", align_bytes=64)
-            if c2 == 0:
-                x_ps[n] = psum.tile([P, S], F32, name="x_ps", bufs=2)
             words = sc_bf[n][:].bitcast(F32)
-            for u in range(2):
-                nc.tensor.transpose(x_ps[n][:, u * 256 + c2 * P:u * 256 + (c2 + 1) * P],
+            for u in range(cp + 1):
+                nc.tensor.transpose(x_banks[cp][:, u * 256 + c2 * P:u * 256 + (c2 + 1) * P],
                                     words[:, c * 256 + u * P:c * 256 + (u + 1) * P], ident_f[:])
             if c2 == 1:
                 gw = grouped[n][:].bitcast(F32)
                 nc.scalar.copy(
                     out=gw[:, cp * S:(cp + 1) * S].rearrange("p (x u) -> p x u", u=2),
-                    in_=x_ps[n][:].rearrange("p (u x) -> p x u", u=2))
+                    in_=x_banks[cp][:].rearrange("p (u x) -> p x u", u=2))
 
         def quant(n):
             codes[n] = work.tile([P, S], U32, name="codes", bufs=4, align_bytes=64)
@@ -153,7 +164,8 @@ def tile_parallelretention_fast3_pa_t_kernel(tc, q_scaled, k, v, omask, out):
                 cols = slice(c * P, (c + 1) * P)
                 nc.scalar.activation(out=o_sb[:, cols], in_=o_ps[:, cols], func=ACT.Copy,
                                      scale=rp[g][:, 4 * h + c:4 * h + c + 1])
-            nc.scalar.dma_start(out=out[g, h].rearrange("(p c) d -> p (c d)", c=4), in_=o_sb[:])
+            nc.scalar.dma_start(out=out[g, h].rearrange("(c p) d -> p c d", p=P),
+                                in_=o_sb[:].rearrange("p (c d) -> p c d", c=4))
 
         for n in range(LAG_T):
             for part in range(4):

@@ -1,8 +1,6 @@
 from contextlib import ExitStack
 
-import concourse.bass as bass
 import concourse.mybir as mybir
-import concourse.tile as tile
 from concourse.masks import make_identity
 
 BF16 = mybir.dt.bfloat16
@@ -18,7 +16,11 @@ P = 128
 NH = B * H
 FLOPS = NH * 2 * (2 * S * S * D)
 
+HEADS = [(2 * pair + i, h) for pair in range(B // 2) for h in range(H) for i in range(2)]
+GROUP = 4
+
 LAG_T = 2
+LAG_V = 3
 LAG_X = 1
 LAG_Q = 2
 LAG_O = 4
@@ -38,12 +40,13 @@ def tile_parallelretention_fast3_pa_t_kernel(tc, q_scaled, k, v, omask, out):
         make_identity(nc, ident_f[:])
 
         q_sb, k_sb, v_sb, om_sb, vcodes, vscales = [], [], [], [], [], []
-        for g in range(B):
-            q_sb.append(res.tile([P, H * 4, D], BF16, name="q_sb%d" % g))
-            k_sb.append(res.tile([P, H * 4, D], BF16, name="k_sb%d" % g))
-            v_sb.append(res.tile([P, H * 2, 2 * D], BF16, name="v_sb%d" % g))
-            vcodes.append(res.tile([P, H * D], U32, name="vcodes%d" % g, align_bytes=64))
-            vscales.append(res.tile([P, H * D], U8, name="vscales%d" % g, align_bytes=64))
+        for b in range(B):
+            q_sb.append(res.tile([P, H * 4, D], BF16, name="q_sb%d" % b))
+            k_sb.append(res.tile([P, H * 4, D], BF16, name="k_sb%d" % b))
+            v_sb.append(res.tile([P, H * 2, 2 * D], BF16, name="v_sb%d" % b))
+        for g in range(NH // GROUP):
+            vcodes.append(res.tile([P, GROUP * D], U32, name="vcodes%d" % g, align_bytes=64))
+            vscales.append(res.tile([P, GROUP * D], U8, name="vscales%d" % g, align_bytes=64))
         for h in range(H):
             om_sb.append(res.tile([P, 4, S], BF16, name="om_sb%d" % h))
 
@@ -59,46 +62,54 @@ def tile_parallelretention_fast3_pa_t_kernel(tc, q_scaled, k, v, omask, out):
         for u in range(2):
             nc.tensor.transpose(x_banks[0][:, 256 + u * P:256 + (u + 1) * P], zero_f[:], ident_f[:])
 
-        for h in range(H):
-            nc.sync.dma_start(out=k_sb[0][:, 4 * h:4 * h + 4, :],
-                              in_=k[0, h].rearrange("(m r) d -> r m d", r=P))
-            nc.sync.dma_start(out=q_sb[0][:, 4 * h:4 * h + 4, :],
-                              in_=q_scaled[0, h].rearrange("(c p) d -> p c d", p=P))
-            nc.sync.dma_start(out=om_sb[h][:],
-                              in_=omask[0, h].rearrange("(c p) j -> p c j", p=P))
-        nc.sync.dma_start(out=v_sb[0][:],
-                          in_=v[0].rearrange("h (u p e) d -> p (h u) (e d)", u=2, e=2))
-        for g in range(1, B):
-            nc.sync.dma_start(out=k_sb[g][:],
-                              in_=k[g].rearrange("h (m r) d -> r (h m) d", r=P))
-            nc.sync.dma_start(out=q_sb[g][:],
-                              in_=q_scaled[g].rearrange("h (c p) d -> p (h c) d", p=P))
-            nc.sync.dma_start(out=v_sb[g][:],
-                              in_=v[g].rearrange("h (u p e) d -> p (h u) (e d)", u=2, e=2))
+        def load_mask(h):
+            for c in range(4):
+                nc.sync.dma_start(out=om_sb[h][:, c, 0:(c + 1) * P],
+                                  in_=omask[0, h, c * P:(c + 1) * P, 0:(c + 1) * P])
+
+        def load_qk(b, h):
+            nc.sync.dma_start(out=k_sb[b][:, 4 * h:4 * h + 4, :],
+                              in_=k[b, h].rearrange("(m r) d -> r m d", r=P))
+            nc.sync.dma_start(out=q_sb[b][:, 4 * h:4 * h + 4, :],
+                              in_=q_scaled[b, h].rearrange("(c p) d -> p c d", p=P))
+
+        def load_v(b, h):
+            nc.sync.dma_start(out=v_sb[b][:, 2 * h:2 * h + 2, :],
+                              in_=v[b, h].rearrange("(u p e) d -> p u (e d)", u=2, e=2))
+
+        for n in range(NH):
+            b, h = HEADS[n]
+            load_qk(b, h)
+            if b == 0:
+                load_mask(h)
+            if b % 2 == 1:
+                load_v(b - 1, h)
+                load_v(b, h)
 
         qkT, sc_bf, grouped, codes, scales, rs, rp, vg = {}, {}, {}, {}, {}, {}, {}, {}
         qk_ps = {}
 
         def t_qk(n, part):
-            g, h = divmod(n, H)
+            b, h = HEADS[n]
             if part == 0:
                 qk_ps[n] = psum.tile([P, 2 * S], BF16, name="qk_ps", bufs=2)
             for idx in (2 * part, 2 * part + 1):
                 if idx < 4:
-                    src = k_sb[g][:, 4 * h + idx, :]
+                    src = k_sb[b][:, 4 * h + idx, :]
                 else:
-                    src = q_sb[g][:, 4 * h + idx - 4, :]
+                    src = q_sb[b][:, 4 * h + idx - 4, :]
                 nc.tensor.transpose(qk_ps[n][:, idx * P:(idx + 1) * P], src, ident_b[:])
             if part == 3:
                 qkT[n] = work.tile([P, 2 * S], BF16, name="qkT")
-                nc.scalar.copy(out=qkT[n][:], in_=qk_ps[n][:])
+                nc.scalar.copy(out=qkT[n][:].bitcast(F32), in_=qk_ps[n][:].bitcast(F32))
 
         def score(n, c):
-            g, h = divmod(n, H)
+            g, j = divmod(n, GROUP)
+            h = HEADS[n][1]
             if c == 0:
                 sc_bf[n] = sc_tiles[n % 3]
-                if h == 0:
-                    rs[g] = work.tile([P, 4 * H], F32, name="rs")
+                if j == 0:
+                    rs[g] = work.tile([P, 4 * GROUP], F32, name="rs")
             s_ps = psum.tile([P, S], F32, name="s_ps", bufs=3)
             keys = (c + 1) * P
             nc.tensor.matmul(out=s_ps[:, 0:keys], lhsT=qkT[n][:, S + c * P:S + (c + 1) * P],
@@ -106,7 +117,7 @@ def tile_parallelretention_fast3_pa_t_kernel(tc, q_scaled, k, v, omask, out):
             nc.vector.scalar_tensor_tensor(
                 out=sc_bf[n][:, c * S:c * S + keys], in0=s_ps[:, 0:keys], scalar=1.0,
                 in1=om_sb[h][:, c, 0:keys], op0=ALU.mult, op1=ALU.mult,
-                accum_out=rs[g][:, 4 * h + c:4 * h + c + 1])
+                accum_out=rs[g][:, 4 * j + c:4 * j + c + 1])
 
         def t_sc(n, c):
             cp, c2 = divmod(c, 2)
@@ -129,11 +140,12 @@ def tile_parallelretention_fast3_pa_t_kernel(tc, q_scaled, k, v, omask, out):
                                   in_=grouped[n][:])
 
         def v_regroup(n):
-            g, h = divmod(n, H)
-            if h == 0:
-                vg[g] = work.tile([P, H, D, 4], BF16, name="vg", bufs=2, align_bytes=64)
-            src = v_sb[g][:, 2 * h:2 * h + 2, :].rearrange("p u (e d) -> p d (u e)", e=2)
-            nc.gpsimd.tensor_scalar(out=vg[g][:, h, :, :], in0=src, scalar1=1.0, scalar2=0.0,
+            g, j = divmod(n, GROUP)
+            b, h = HEADS[n]
+            if j == 0:
+                vg[g] = work.tile([P, GROUP, D, 4], BF16, name="vg", bufs=2, align_bytes=64)
+            src = v_sb[b][:, 2 * h:2 * h + 2, :].rearrange("p u (e d) -> p d (u e)", e=2)
+            nc.gpsimd.tensor_scalar(out=vg[g][:, j, :, :], in0=src, scalar1=1.0, scalar2=0.0,
                                     op0=ALU.mult, op1=ALU.add)
 
         def v_quant(g):
@@ -141,35 +153,36 @@ def tile_parallelretention_fast3_pa_t_kernel(tc, q_scaled, k, v, omask, out):
                                   in_=vg[g][:].rearrange("p h d t -> p (h d t)"))
 
         def p_ops(g):
-            ab = work.tile([P, 4 * H], F32, name="ab")
-            rp[g] = work.tile([P, 4 * H], F32, name="rp")
+            ab = work.tile([P, 4 * GROUP], F32, name="ab")
+            rp[g] = work.tile([P, 4 * GROUP], F32, name="rp")
             nc.vector.scalar_tensor_tensor(out=ab[:], in0=rs[g][:], scalar=-1.0, in1=rs[g][:],
                                            op0=ALU.mult, op1=ALU.max)
             nc.vector.tensor_scalar_max(out=ab[:], in0=ab[:], scalar1=1.0)
             nc.vector.reciprocal(out=rp[g][:], in_=ab[:])
 
         def output(n):
-            g, h = divmod(n, H)
+            g, j = divmod(n, GROUP)
+            b, h = HEADS[n]
             o_ps = psum.tile([P, S], F32, name="o_ps", bufs=1)
             for c in range(4):
                 cols = slice(c * P, (c + 1) * P)
                 nc.tensor.matmul_mx(out=o_ps[:, cols],
                                     lhsT=codes[n][:, cols].bitcast(FP8X4),
                                     lhsT_scale=scales[n][:, cols],
-                                    rhs=vcodes[g][:, h * D:(h + 1) * D].bitcast(FP8X4),
-                                    rhs_scale=vscales[g][:, h * D:(h + 1) * D],
+                                    rhs=vcodes[g][:, j * D:(j + 1) * D].bitcast(FP8X4),
+                                    rhs_scale=vscales[g][:, j * D:(j + 1) * D],
                                     start=True, stop=True)
             o_sb = work.tile([P, S], F32, name="o_sb", bufs=4)
             for c in range(4):
                 cols = slice(c * P, (c + 1) * P)
                 nc.scalar.activation(out=o_sb[:, cols], in_=o_ps[:, cols], func=ACT.Copy,
-                                     scale=rp[g][:, 4 * h + c:4 * h + c + 1])
-            nc.scalar.dma_start(out=out[g, h].rearrange("(c p) d -> p c d", p=P),
+                                     scale=rp[g][:, 4 * j + c:4 * j + c + 1])
+            nc.scalar.dma_start(out=out[b, h].rearrange("(c p) d -> p c d", p=P),
                                 in_=o_sb[:].rearrange("p (c d) -> p c d", c=4))
 
-        for n in range(LAG_T):
-            for part in range(4):
-                t_qk(n, part)
+        for part in range(4):
+            t_qk(0, part)
+        for n in range(LAG_V):
             v_regroup(n)
 
         for step in range(NH + LAG_O):
@@ -178,14 +191,17 @@ def tile_parallelretention_fast3_pa_t_kernel(tc, q_scaled, k, v, omask, out):
             for c in range(4):
                 if step < NH:
                     score(step, c)
+                if step == 0:
+                    t_qk(1, c)
                 if step + LAG_T < NH:
                     t_qk(step + LAG_T, c)
                 if 0 <= step - LAG_X < NH:
                     t_sc(step - LAG_X, c)
-            if step + 2 < NH:
-                v_regroup(step + 2)
+            if step + LAG_V < NH:
+                v_regroup(step + LAG_V)
             if 0 <= step - LAG_Q < NH:
                 quant(step - LAG_Q)
-            if step < NH and step % H == H - 1:
-                v_quant(step // H)
-                p_ops(step // H)
+            if step < NH and step % GROUP == GROUP - 2:
+                v_quant(step // GROUP)
+            if step < NH and step % GROUP == GROUP - 1:
+                p_ops(step // GROUP)

@@ -6,6 +6,7 @@ from concourse.masks import make_identity
 BF16 = mybir.dt.bfloat16
 F32 = mybir.dt.float32
 U32 = mybir.dt.uint32
+I32 = mybir.dt.int32
 U8 = mybir.dt.uint8
 FP8X4 = mybir.dt.float8_e4m3fn_x4
 ALU = mybir.AluOpType
@@ -18,12 +19,13 @@ FLOPS = NH * 2 * (2 * S * S * D)
 
 HEADS = [(2 * pair + i, h) for pair in range(B // 2) for h in range(H) for i in range(2)]
 GROUP = 4
+NG = NH // GROUP
+NP = NG // 2
 
 LAG_T = 2
-LAG_V = 3
+LAG_V = 6
 LAG_X = 1
 LAG_Q = 2
-LAG_O = 4
 
 
 def tile_parallelretention_fast3_pa_t_kernel(tc, q_scaled, k, v, omask, out):
@@ -34,8 +36,12 @@ def tile_parallelretention_fast3_pa_t_kernel(tc, q_scaled, k, v, omask, out):
         work = ctx.enter_context(tc.tile_pool(name="work", bufs=3))
         psum = ctx.enter_context(tc.psum_pool(name="psum", bufs=1))
 
+        ctx.enter_context(tc.manual_schedule())
         ident_b = const.tile([P, P], BF16, name="ident_b")
         make_identity(nc, ident_b[:])
+        perm_b = const.tile([P, P], BF16, name="perm_b")
+        nc.vector.tensor_copy(out=perm_b[:].rearrange("i (u p e) -> i u p e", u=2, e=2),
+                              in_=ident_b[:].rearrange("i (p u e) -> i u p e", u=2, e=2))
         ident_f = const.tile([P, P], F32, name="ident_f")
         make_identity(nc, ident_f[:])
 
@@ -43,114 +49,174 @@ def tile_parallelretention_fast3_pa_t_kernel(tc, q_scaled, k, v, omask, out):
         for b in range(B):
             q_sb.append(res.tile([P, H * 4, D], BF16, name="q_sb%d" % b))
             k_sb.append(res.tile([P, H * 4, D], BF16, name="k_sb%d" % b))
-            v_sb.append(res.tile([P, H * 2, 2 * D], BF16, name="v_sb%d" % b))
-        for g in range(NH // GROUP):
-            vcodes.append(res.tile([P, GROUP * D], U32, name="vcodes%d" % g, align_bytes=64))
-            vscales.append(res.tile([P, GROUP * D], U8, name="vscales%d" % g, align_bytes=64))
+            v_sb.append(res.tile([P, H, 4 * D], BF16, name="v_sb%d" % b))
+        for p in range(NP):
+            vcodes.append(res.tile([P, 2 * GROUP, D], U32, name="vcodes%d" % p, align_bytes=64))
+            vscales.append(res.tile([P, 2 * GROUP, D], U8, name="vscales%d" % p, align_bytes=64))
         for h in range(H):
             om_sb.append(res.tile([P, 4, S], BF16, name="om_sb%d" % h))
 
-        sc_tiles = []
+        ab_tiles = []
         for i in range(3):
-            t = res.tile([P, 4 * S], BF16, name="sc_tile%d" % i)
-            nc.vector.memset(t[:, P:2 * P], 0.0)
-            nc.vector.memset(t[:, 2 * S + 3 * P:3 * S], 0.0)
-            sc_tiles.append(t)
-        zero_f = const.tile([P, P], F32, name="zero_f")
-        nc.vector.memset(zero_f[:], 0.0)
-        x_banks = [psum.tile([P, S], F32, name="x_bank%d" % i) for i in range(2)]
-        for u in range(2):
-            nc.tensor.transpose(x_banks[0][:, 256 + u * P:256 + (u + 1) * P], zero_f[:], ident_f[:])
+            t = res.tile([P, 2, 2, 2 * P], BF16, name="ab_tile%d" % i)
+            nc.vector.memset(t[:, 1, :, 192:256], 0.0)
+            ab_tiles.append(t)
+        vc_codes, vc_scales, vd_codes, vd_scales, zeroed = [], [], [], [], []
+        for i in range(2):
+            for (cl, sl, nm) in ((vc_codes, vc_scales, "vc"), (vd_codes, vd_scales, "vd")):
+                t = res.tile([P, 2 * GROUP, D], U32, name="%s_codes%d" % (nm, i), align_bytes=64)
+                zeroed.append(t[:].bitcast(I32))
+                cl.append(t)
+                t2 = res.tile([P, 2 * GROUP, D], U8, name="%s_scales%d" % (nm, i), align_bytes=64)
+                zeroed.append(t2[:].rearrange("p h d -> p (h d)").bitcast(I32))
+                sl.append(t2)
+
+        def order_mask(h):
+            for c in range(4):
+                keys = (c + 1) * P
+                dst = om_sb[h][:, c, 0:keys].rearrange("q (u p e) -> q u p e", u=2, e=2)
+                src = om_raw[h][:, c, 0:keys].rearrange("q (p u e) -> q u p e", u=2, e=2)
+                if h == 0:
+                    nc.vector.tensor_copy(out=dst, in_=src)
+                else:
+                    nc.gpsimd.tensor_scalar(out=dst, in0=src, scalar1=1.0, scalar2=0.0,
+                                            op0=ALU.mult, op1=ALU.add)
+
+        om_raw = {}
+
+        def load_k(b, h, nh):
+            nc.sync.dma_start(out=k_sb[b][:, 4 * h:4 * (h + nh), :],
+                              in_=k[b, h:h + nh].rearrange("h (a r) d -> r (h a) d", r=P))
+
+        def load_q(b, h, nh):
+            nc.sync.dma_start(out=q_sb[b][:, 4 * h:4 * (h + nh), :],
+                              in_=q_scaled[b, h:h + nh].rearrange("h (c p) d -> p (h c) d", p=P))
+
+        def load_v(b, h, nh):
+            nc.sync.dma_start(out=v_sb[b][:, h:h + nh, :],
+                              in_=v[b, h:h + nh].rearrange("h (p t) d -> p h (t d)", t=4))
 
         def load_mask(h):
+            om_raw[h] = work.tile([P, 4, S], BF16, name="om_raw", bufs=4)
             for c in range(4):
-                nc.sync.dma_start(out=om_sb[h][:, c, 0:(c + 1) * P],
+                nc.sync.dma_start(out=om_raw[h][:, c, 0:(c + 1) * P],
                                   in_=omask[0, h, c * P:(c + 1) * P, 0:(c + 1) * P])
 
-        def load_qk(b, h):
-            nc.sync.dma_start(out=k_sb[b][:, 4 * h:4 * h + 4, :],
-                              in_=k[b, h].rearrange("(m r) d -> r m d", r=P))
-            nc.sync.dma_start(out=q_sb[b][:, 4 * h:4 * h + 4, :],
-                              in_=q_scaled[b, h].rearrange("(c p) d -> p c d", p=P))
+        def load_part(p, part):
+            b = 2 * p + part % 2
+            (load_v, load_k, load_q)[part // 2](b, 0, H)
 
-        def load_v(b, h):
-            nc.sync.dma_start(out=v_sb[b][:, 2 * h:2 * h + 2, :],
-                              in_=v[b, h].rearrange("(u p e) d -> p u (e d)", u=2, e=2))
-
-        for n in range(NH):
-            b, h = HEADS[n]
-            load_qk(b, h)
-            if b == 0:
-                load_mask(h)
-            if b % 2 == 1:
-                load_v(b - 1, h)
-                load_v(b, h)
-
-        qkT, sc_bf, grouped, codes, scales, rs, rp, vg = {}, {}, {}, {}, {}, {}, {}, {}
-        qk_ps = {}
+        qkT, sc_c, sc_d = {}, {}, {}
+        gab, gc0, gc1d = {}, {}, {}
+        codes, scales, codes0, scales0, codes1, scales1 = {}, {}, {}, {}, {}, {}
+        rs, rp, vg, o_sb, qk_ps = {}, {}, {}, {}, {}
 
         def t_qk(n, part):
             b, h = HEADS[n]
             if part == 0:
-                qk_ps[n] = psum.tile([P, 2 * S], BF16, name="qk_ps", bufs=2)
-            for idx in (2 * part, 2 * part + 1):
+                qk_ps[n] = psum.tile([P, 2 * S], BF16, name="qk_ps")
+            for idx in range(4 * part, 4 * part + 4):
                 if idx < 4:
-                    src = k_sb[b][:, 4 * h + idx, :]
+                    dst = qk_ps[n][:, 0:S].rearrange("d (u a x) -> d a u x", u=2, a=4)[:, idx, :, :]
+                    nc.tensor.transpose(dst, k_sb[b][:, 4 * h + idx, :], perm_b[:])
                 else:
-                    src = q_sb[b][:, 4 * h + idx - 4, :]
-                nc.tensor.transpose(qk_ps[n][:, idx * P:(idx + 1) * P], src, ident_b[:])
-            if part == 3:
+                    nc.tensor.transpose(qk_ps[n][:, idx * P:(idx + 1) * P],
+                                        q_sb[b][:, 4 * h + idx - 4, :], ident_b[:])
+            if part == 1:
                 qkT[n] = work.tile([P, 2 * S], BF16, name="qkT")
                 nc.scalar.copy(out=qkT[n][:].bitcast(F32), in_=qk_ps[n][:].bitcast(F32))
 
         def score(n, c):
             g, j = divmod(n, GROUP)
             h = HEADS[n][1]
-            if c == 0:
-                sc_bf[n] = sc_tiles[n % 3]
-                if j == 0:
-                    rs[g] = work.tile([P, 4 * GROUP], F32, name="rs")
+            if g not in rs:
+                rs[g] = work.tile([P, 4 * GROUP], F32, name="rs")
+                sc_c[g] = work.tile([P, 2, 2, 2 * P], BF16, name="sc_c", bufs=2)
+                sc_d[g] = work.tile([P, 2, 2 * P], BF16, name="sc_d", bufs=2)
             s_ps = psum.tile([P, S], F32, name="s_ps", bufs=3)
-            keys = (c + 1) * P
-            nc.tensor.matmul(out=s_ps[:, 0:keys], lhsT=qkT[n][:, S + c * P:S + (c + 1) * P],
-                             rhs=qkT[n][:, 0:keys], start=True, stop=True)
+            half = 64 * (c + 1)
+            sc = s_ps[:, 0:2 * half].rearrange("q (u x) -> q u x", u=2)
+            nc.tensor.matmul(out=sc, lhsT=qkT[n][:, S + c * P:S + (c + 1) * P],
+                             rhs=qkT[n][:, 0:S].rearrange("d (u x) -> d u x", u=2)[:, :, 0:half],
+                             start=True, stop=True)
+            if c == 3:
+                dst = ab_tiles[n % 3][:, 0, :, :]
+            elif c == 2:
+                dst = ab_tiles[n % 3][:, 1, :, 0:half]
+            elif c == 1:
+                dst = sc_c[g][:, j // 2, :, (j % 2) * half:(j % 2 + 1) * half]
+            else:
+                dst = sc_d[g][:, :, j * half:(j + 1) * half]
             nc.vector.scalar_tensor_tensor(
-                out=sc_bf[n][:, c * S:c * S + keys], in0=s_ps[:, 0:keys], scalar=1.0,
-                in1=om_sb[h][:, c, 0:keys], op0=ALU.mult, op1=ALU.mult,
-                accum_out=rs[g][:, 4 * j + c:4 * j + c + 1])
+                out=dst, in0=sc, scalar=1.0,
+                in1=om_sb[h][:, c, 0:2 * half].rearrange("q (u x) -> q u x", u=2),
+                op0=ALU.mult, op1=ALU.mult, accum_out=rs[g][:, 4 * j + c:4 * j + c + 1])
 
-        def t_sc(n, c):
-            cp, c2 = divmod(c, 2)
-            if c == 0:
-                grouped[n] = work.tile([P, 4 * S], BF16, name="grouped", align_bytes=64)
-            words = sc_bf[n][:].bitcast(F32)
-            for u in range(cp + 1):
-                nc.tensor.transpose(x_banks[cp][:, u * 256 + c2 * P:u * 256 + (c2 + 1) * P],
-                                    words[:, c * 256 + u * P:c * 256 + (u + 1) * P], ident_f[:])
-            if c2 == 1:
-                gw = grouped[n][:].bitcast(F32)
-                nc.scalar.copy(
-                    out=gw[:, cp * S:(cp + 1) * S].rearrange("p (x u) -> p x u", u=2),
-                    in_=x_banks[cp][:].rearrange("p (u x) -> p x u", u=2))
+        def t_slot(bank, slot, nslots, src):
+            words = src.rearrange("q u x -> q (u x)").bitcast(F32)
+            for u in range(2):
+                nc.tensor.transpose(bank[:, (u * nslots + slot) * P:(u * nslots + slot + 1) * P],
+                                    words[:, u * P:(u + 1) * P], ident_f[:])
 
-        def quant(n):
-            codes[n] = work.tile([P, S], U32, name="codes", bufs=4, align_bytes=64)
-            scales[n] = work.tile([P, S], U8, name="scales", bufs=4, align_bytes=64)
-            nc.vector.quantize_mx(out=codes[n][:].bitcast(FP8X4), scales=scales[n][:],
-                                  in_=grouped[n][:])
+        def x_out(dst, bank, nslots):
+            nc.scalar.copy(out=dst[:].bitcast(F32).rearrange("p (x u) -> p x u", u=2),
+                           in_=bank[:, 0:nslots * 256].rearrange("p (u x) -> p x u", u=2))
+
+        def t_ab(n):
+            x_ab = psum.tile([P, S], F32, name="x_ps", bufs=2)
+            for slot in range(2):
+                t_slot(x_ab, slot, 2, ab_tiles[n % 3][:, slot, :, :])
+            gab[n] = work.tile([P, 2 * S], BF16, name="gab", align_bytes=64)
+            x_out(gab[n], x_ab, 2)
+
+        def t_c0(g):
+            x_cd = psum.tile([P, S], F32, name="x_ps", bufs=2)
+            t_slot(x_cd, 0, 1, sc_c[g][:, 0, :, :])
+            gc0[g] = work.tile([P, S], BF16, name="gc0", bufs=2, align_bytes=64)
+            x_out(gc0[g], x_cd, 1)
+
+        def t_c1d(g):
+            x_cd = psum.tile([P, S], F32, name="x_ps", bufs=2)
+            t_slot(x_cd, 0, 2, sc_c[g][:, 1, :, :])
+            t_slot(x_cd, 1, 2, sc_d[g][:])
+            gc1d[g] = work.tile([P, 2 * S], BF16, name="gc1d", bufs=2, align_bytes=64)
+            x_out(gc1d[g], x_cd, 2)
+
+        def quant(dst_codes, dst_scales, key, src, width, nm, bufs):
+            dst_codes[key] = work.tile([P, width], U32, name="codes_" + nm, bufs=bufs, align_bytes=64)
+            dst_scales[key] = work.tile([P, width], U8, name="scales_" + nm, bufs=bufs, align_bytes=64)
+            nc.vector.quantize_mx(out=dst_codes[key][:].bitcast(FP8X4), scales=dst_scales[key][:],
+                                  in_=src[key][:])
 
         def v_regroup(n):
             g, j = divmod(n, GROUP)
             b, h = HEADS[n]
             if j == 0:
                 vg[g] = work.tile([P, GROUP, D, 4], BF16, name="vg", bufs=2, align_bytes=64)
-            src = v_sb[b][:, 2 * h:2 * h + 2, :].rearrange("p u (e d) -> p d (u e)", e=2)
-            nc.gpsimd.tensor_scalar(out=vg[g][:, j, :, :], in0=src, scalar1=1.0, scalar2=0.0,
-                                    op0=ALU.mult, op1=ALU.add)
+            nc.gpsimd.tensor_scalar(out=vg[g][:, j, :, :],
+                                    in0=v_sb[b][:, h, :].rearrange("p (t d) -> p d t", t=4),
+                                    scalar1=1.0, scalar2=0.0, op0=ALU.mult, op1=ALU.add)
+
+        def v_of(tiles, g):
+            return tiles[g // 2][:, GROUP * (g % 2):GROUP * (g % 2 + 1), :]
 
         def v_quant(g):
-            nc.vector.quantize_mx(out=vcodes[g][:].bitcast(FP8X4), scales=vscales[g][:],
+            nc.vector.quantize_mx(out=v_of(vcodes, g).rearrange("p h d -> p (h d)").bitcast(FP8X4),
+                                  scales=v_of(vscales, g).rearrange("p h d -> p (h d)"),
                                   in_=vg[g][:].rearrange("p h d t -> p (h d t)"))
+
+        def v_move(p):
+            vc, vs = vcodes[p][:].bitcast(I32), vscales[p][:].bitcast(I32)
+            c_codes, c_scales = vc_codes[p % 2][:].bitcast(I32), vc_scales[p % 2][:].bitcast(I32)
+            d_codes, d_scales = vd_codes[p % 2][:].bitcast(I32), vd_scales[p % 2][:].bitcast(I32)
+            for i in range(2):
+                nc.sync.dma_start(out=c_codes[64 * i:64 * i + 64, i::2, :], in_=vc[0:64, i::2, :])
+                for r in (0, 32):
+                    nc.sync.dma_start(out=c_scales[64 * i + r:64 * i + r + 4, i::2, :],
+                                      in_=vs[r:r + 4, i::2, :])
+            for j in range(GROUP):
+                nc.sync.dma_start(out=d_codes[32 * j:32 * j + 32, j::GROUP, :], in_=vc[0:32, j::GROUP, :])
+                nc.sync.dma_start(out=d_scales[32 * j:32 * j + 4, j::GROUP, :], in_=vs[0:4, j::GROUP, :])
 
         def p_ops(g):
             ab = work.tile([P, 4 * GROUP], F32, name="ab")
@@ -160,48 +226,165 @@ def tile_parallelretention_fast3_pa_t_kernel(tc, q_scaled, k, v, omask, out):
             nc.vector.tensor_scalar_max(out=ab[:], in0=ab[:], scalar1=1.0)
             nc.vector.reciprocal(out=rp[g][:], in_=ab[:])
 
-        def output(n):
+        def packed(tiles, g):
+            return tiles[g // 2 % 2][:, GROUP * (g % 2):GROUP * (g % 2 + 1), :]
+
+        def mx(o, lc, ls, rc, rsc):
+            nc.tensor.matmul_mx(out=o, lhsT=lc.bitcast(FP8X4), lhsT_scale=ls, rhs=rc.bitcast(FP8X4),
+                                rhs_scale=rsc, start=True, stop=True)
+
+        def scaled(n, c, src, on_vector):
             g, j = divmod(n, GROUP)
-            b, h = HEADS[n]
-            o_ps = psum.tile([P, S], F32, name="o_ps", bufs=1)
-            for c in range(4):
-                cols = slice(c * P, (c + 1) * P)
-                nc.tensor.matmul_mx(out=o_ps[:, cols],
-                                    lhsT=codes[n][:, cols].bitcast(FP8X4),
-                                    lhsT_scale=scales[n][:, cols],
-                                    rhs=vcodes[g][:, j * D:(j + 1) * D].bitcast(FP8X4),
-                                    rhs_scale=vscales[g][:, j * D:(j + 1) * D],
-                                    start=True, stop=True)
-            o_sb = work.tile([P, S], F32, name="o_sb", bufs=4)
-            for c in range(4):
-                cols = slice(c * P, (c + 1) * P)
-                nc.scalar.activation(out=o_sb[:, cols], in_=o_ps[:, cols], func=ACT.Copy,
-                                     scale=rp[g][:, 4 * j + c:4 * j + c + 1])
-            nc.scalar.dma_start(out=out[b, h].rearrange("(c p) d -> p c d", p=P),
-                                in_=o_sb[:].rearrange("p (c d) -> p c d", c=4))
+            factor = rp[g][:, 4 * j + c:4 * j + c + 1]
+            dst = o_sb[g, j % 2][:, j // 2, c, :]
+            if on_vector:
+                nc.vector.tensor_scalar_mul(out=dst, in0=src, scalar1=factor)
+            else:
+                nc.scalar.activation(out=dst, in_=src, func=ACT.Copy, scale=factor)
 
-        for part in range(4):
+        def out_ab(n0, on_vector):
+            g = n0 // GROUP
+            o_ps = psum.tile([P, S], F32, name="o_ps", bufs=2)
+            parts = [(n0 + i // 2, 3 - i % 2) for i in range(4)]
+            for i, (n, c) in enumerate(parts):
+                slot = slice((3 - c) * P, (4 - c) * P)
+                mx(o_ps[:, i * P:(i + 1) * P], codes[n][:, slot], scales[n][:, slot],
+                   v_of(vcodes, g)[:, n % GROUP, :], v_of(vscales, g)[:, n % GROUP, :])
+            if n0 % GROUP == 0:
+                for i in range(2):
+                    o_sb[g, i] = work.tile([P, 2, 4, D], F32, name="o_sb", bufs=4)
+            for i, (n, c) in enumerate(parts):
+                scaled(n, c, o_ps[:, i * P:(i + 1) * P], on_vector)
+
+        def out_c(g, on_vector):
+            o_ps = psum.tile([P, S], F32, name="o_ps", bufs=2)
+            for i, (lc, ls) in enumerate(((codes0[g], scales0[g]), (codes1[g], scales1[g]))):
+                mx(o_ps[:, i * 256:(i + 1) * 256], lc[:, 0:P], ls[:, 0:P],
+                   packed(vc_codes, g)[:, 2 * i:2 * i + 2, :].rearrange("p h d -> p (h d)"),
+                   packed(vc_scales, g)[:, 2 * i:2 * i + 2, :].rearrange("p h d -> p (h d)"))
+            for j in range(GROUP):
+                scaled(GROUP * g + j, 1, o_ps[:, j * P:(j + 1) * P], on_vector)
+
+        def out_d(g, on_vector):
+            o_ps = psum.tile([P, S], F32, name="o_ps", bufs=2)
+            mx(o_ps[:], codes1[g][:, P:2 * P], scales1[g][:, P:2 * P],
+               packed(vd_codes, g).rearrange("p h d -> p (h d)"),
+               packed(vd_scales, g).rearrange("p h d -> p (h d)"))
+            for j in range(GROUP):
+                scaled(GROUP * g + j, 0, o_ps[:, j * P:(j + 1) * P], on_vector)
+
+        def store(g):
+            b, h = HEADS[GROUP * g]
+            for i in range(2):
+                nc.sync.dma_start(out=out[b + i, h:h + 2].rearrange("h (c p) d -> p (h c) d", p=P),
+                                  in_=o_sb[g, i][:].rearrange("p h c d -> p (h c) d"))
+
+        def store_part(g, c0):
+            for j in range(GROUP):
+                b, h = HEADS[GROUP * g + j]
+                nc.sync.dma_start(out=out[b, h].rearrange("(c p) d -> p c d", p=P)[:, c0:c0 + 2, :],
+                                  in_=o_sb[g, j % 2][:, j // 2, c0:c0 + 2, :])
+
+        for h in range(H):
+            for b in range(2):
+                load_k(b, h, 1)
+                load_q(b, h, 1)
+                if b == 0:
+                    load_mask(h)
+            for b in range(2):
+                load_v(b, h, 1)
+        for b in (2, 3):
+            load_v(b, 0, H)
+        for b in (2, 3):
+            load_k(b, 0, 2)
+            load_q(b, 0, 2)
+        for view in zeroed[4:8]:
+            nc.vector.memset(view, 0)
+        order_mask(0)
+        for part in range(2):
             t_qk(0, part)
-        for n in range(LAG_V):
-            v_regroup(n)
+        for view in zeroed[0:4]:
+            nc.gpsimd.memset(view, 0)
+        v_regroup(0)
+        v_regroup(1)
+        order_mask(1)
+        v_regroup(2)
+        v_regroup(3)
+        order_mask(2)
+        v_regroup(4)
+        v_regroup(5)
 
-        for step in range(NH + LAG_O):
-            if 0 <= step - LAG_O < NH:
-                output(step - LAG_O)
-            for c in range(4):
-                if step < NH:
-                    score(step, c)
-                if step == 0:
-                    t_qk(1, c)
-                if step + LAG_T < NH:
-                    t_qk(step + LAG_T, c)
-                if 0 <= step - LAG_X < NH:
-                    t_sc(step - LAG_X, c)
+        for step in range(NH + 1):
+            g, j = divmod(step, GROUP)
+            live = step < NH
+            order = (0, 1, 2, 3) if step == 0 else (3, 2, 1, 0)
+            if live:
+                score(step, order[0])
+            if step == 0:
+                for part in range(2):
+                    t_qk(1, part)
+            if j == 0 and g > 1 and live:
+                out_d(g - 2, False)
+            elif j == 1 and g > 0:
+                out_ab(step - 5, False)
+                if g > 1:
+                    store(g - 2)
+            elif j == 2 and g > 0:
+                out_ab(step - 4, False)
+            elif j == 3 and g > 0:
+                out_c(g - 1, False)
+                if step == NH - 1:
+                    out_d(g - 1, False)
+                    store(g - 1)
+            if live:
+                score(step, order[1])
+            if step + LAG_T < NH:
+                t_qk(step + LAG_T, 0)
+            m = step - LAG_Q
+            if 0 <= m < NH:
+                quant(codes, scales, m, gab, 2 * P, "ab", 6)
+                if m % GROUP == 1:
+                    quant(codes0, scales0, m // GROUP, gc0, P, "c0", 2)
+                if m % GROUP == 3:
+                    quant(codes1, scales1, m // GROUP, gc1d, 2 * P, "c1d", 2)
+            last = step - LAG_X
+            if 0 <= last < NH - 1:
+                t_ab(last)
+            if step == NH - 1:
+                t_ab(step)
+            if live:
+                score(step, order[2])
+            if step + LAG_T < NH:
+                t_qk(step + LAG_T, 1)
+            if 0 <= last < NH and last % GROUP == 1:
+                t_c0(last // GROUP)
+            if 0 <= last < NH and last % GROUP == 3:
+                t_c1d(last // GROUP)
+            if live:
+                score(step, order[3])
             if step + LAG_V < NH:
                 v_regroup(step + LAG_V)
-            if 0 <= step - LAG_Q < NH:
-                quant(step - LAG_Q)
-            if step < NH and step % GROUP == GROUP - 2:
-                v_quant(step // GROUP)
-            if step < NH and step % GROUP == GROUP - 1:
-                p_ops(step // GROUP)
+            if step == 1:
+                order_mask(3)
+            for gg, at in enumerate([2, 4] + [4 * gg - 2 for gg in range(2, NG)]):
+                if step == at:
+                    v_quant(gg)
+                    if gg % 2 == 1:
+                        v_move(gg // 2)
+            if step == 4:
+                for b in (2, 3):
+                    load_k(b, 2, 2)
+                    load_q(b, 2, 2)
+            pair, part = divmod(step - 5, 8)
+            if step >= 5 and part < 6 and pair + 2 < NP:
+                load_part(pair + 2, part)
+            if live and j == GROUP - 1:
+                p_ops(g)
+        out_ab(NH - 4, False)
+        quant(codes, scales, NH - 1, gab, 2 * P, "ab", 6)
+        out_ab(NH - 2, True)
+        store_part(NG - 1, 2)
+        quant(codes1, scales1, NG - 1, gc1d, 2 * P, "c1d", 2)
+        out_c(NG - 1, False)
+        out_d(NG - 1, True)
+        store_part(NG - 1, 0)

@@ -39,16 +39,13 @@ def tile_parallelretention_fast3_pa_t_kernel(tc, q_scaled, k, v, omask, out):
         ctx.enter_context(tc.manual_schedule())
         ident_b = const.tile([P, P], BF16, name="ident_b")
         make_identity(nc, ident_b[:])
-        perm_b = const.tile([P, P], BF16, name="perm_b")
-        nc.vector.tensor_copy(out=perm_b[:].rearrange("i (u p e) -> i u p e", u=2, e=2),
-                              in_=ident_b[:].rearrange("i (p u e) -> i u p e", u=2, e=2))
         ident_f = const.tile([P, P], F32, name="ident_f")
         make_identity(nc, ident_f[:])
 
         q_sb, k_sb, v_sb, om_sb, vcodes, vscales = [], [], [], [], [], []
         for b in range(B):
-            q_sb.append(res.tile([P, H * 4, D], BF16, name="q_sb%d" % b))
-            k_sb.append(res.tile([P, H * 4, D], BF16, name="k_sb%d" % b))
+            q_sb.append(res.tile([P, H * 2, 2 * D], BF16, name="q_sb%d" % b))
+            k_sb.append(res.tile([P, H * 2, 2 * D], BF16, name="k_sb%d" % b))
             v_sb.append(res.tile([P, H, 4 * D], BF16, name="v_sb%d" % b))
         for p in range(NP):
             vcodes.append(res.tile([P, 2 * GROUP, D], U32, name="vcodes%d" % p, align_bytes=64))
@@ -75,7 +72,7 @@ def tile_parallelretention_fast3_pa_t_kernel(tc, q_scaled, k, v, omask, out):
             for c in range(4):
                 keys = (c + 1) * P
                 dst = om_sb[h][:, c, 0:keys].rearrange("q (u p e) -> q u p e", u=2, e=2)
-                src = om_raw[h][:, c, 0:keys].rearrange("q (p u e) -> q u p e", u=2, e=2)
+                src = om_raw[h][:, c, 0:keys].rearrange("q (p e u) -> q u p e", u=2, e=2)
                 if h == 0:
                     nc.vector.tensor_copy(out=dst, in_=src)
                 else:
@@ -85,12 +82,12 @@ def tile_parallelretention_fast3_pa_t_kernel(tc, q_scaled, k, v, omask, out):
         om_raw = {}
 
         def load_k(b, h, nh):
-            nc.sync.dma_start(out=k_sb[b][:, 4 * h:4 * (h + nh), :],
-                              in_=k[b, h:h + nh].rearrange("h (a r) d -> r (h a) d", r=P))
+            nc.sync.dma_start(out=k_sb[b][:, 2 * h:2 * (h + nh), :],
+                              in_=k[b, h:h + nh].rearrange("h (i r m) d -> r (h i) (m d)", i=2, m=2))
 
         def load_q(b, h, nh):
-            nc.sync.dma_start(out=q_sb[b][:, 4 * h:4 * (h + nh), :],
-                              in_=q_scaled[b, h:h + nh].rearrange("h (c p) d -> p (h c) d", p=P))
+            nc.sync.dma_start(out=q_sb[b][:, 2 * h:2 * (h + nh), :],
+                              in_=q_scaled[b, h:h + nh].rearrange("h (i r m) d -> r (h i) (m d)", i=2, m=2))
 
         def load_v(b, h, nh):
             nc.sync.dma_start(out=v_sb[b][:, h:h + nh, :],
@@ -98,9 +95,11 @@ def tile_parallelretention_fast3_pa_t_kernel(tc, q_scaled, k, v, omask, out):
 
         def load_mask(h):
             om_raw[h] = work.tile([P, 4, S], BF16, name="om_raw", bufs=4)
-            for c in range(4):
-                nc.sync.dma_start(out=om_raw[h][:, c, 0:(c + 1) * P],
-                                  in_=omask[0, h, c * P:(c + 1) * P, 0:(c + 1) * P])
+            rows = omask[0, h].rearrange("(c r m) j -> m r c j", r=64, m=2)
+            for i in range(2):
+                for m in range(2):
+                    nc.sync.dma_start(out=om_raw[h][64 * m:64 * m + 64, 2 * i:2 * i + 2, 0:256 * (i + 1)],
+                                      in_=rows[m, :, 2 * i:2 * i + 2, 0:256 * (i + 1)])
 
         def load_part(p, part):
             b = 2 * p + part % 2
@@ -116,12 +115,15 @@ def tile_parallelretention_fast3_pa_t_kernel(tc, q_scaled, k, v, omask, out):
             if part == 0:
                 qk_ps[n] = psum.tile([P, 2 * S], BF16, name="qk_ps")
             for idx in range(4 * part, 4 * part + 4):
+                i, m = divmod(idx % 4, 2)
                 if idx < 4:
-                    dst = qk_ps[n][:, 0:S].rearrange("d (u a x) -> d a u x", u=2, a=4)[:, idx, :, :]
-                    nc.tensor.transpose(dst, k_sb[b][:, 4 * h + idx, :], perm_b[:])
+                    dst = qk_ps[n][:, 256 * m + P * i:256 * m + P * (i + 1)]
+                    src = k_sb[b]
                 else:
-                    nc.tensor.transpose(qk_ps[n][:, idx * P:(idx + 1) * P],
-                                        q_sb[b][:, 4 * h + idx - 4, :], ident_b[:])
+                    dst = qk_ps[n][:, S + 256 * i:S + 256 * (i + 1)].rearrange(
+                        "d (c m r) -> d m c r", c=2, m=2)[:, m, :, :]
+                    src = q_sb[b]
+                nc.tensor.transpose(dst, src[:, 2 * h + i, m * D:(m + 1) * D], ident_b[:])
             if part == 1:
                 qkT[n] = work.tile([P, 2 * S], BF16, name="qkT")
                 nc.scalar.copy(out=qkT[n][:].bitcast(F32), in_=qk_ps[n][:].bitcast(F32))
@@ -193,8 +195,8 @@ def tile_parallelretention_fast3_pa_t_kernel(tc, q_scaled, k, v, omask, out):
             b, h = HEADS[n]
             if j == 0:
                 vg[g] = work.tile([P, GROUP, D, 4], BF16, name="vg", bufs=2, align_bytes=64)
-            nc.gpsimd.tensor_scalar(out=vg[g][:, j, :, :],
-                                    in0=v_sb[b][:, h, :].rearrange("p (t d) -> p d t", t=4),
+            nc.gpsimd.tensor_scalar(out=vg[g][:, j, :, :].rearrange("p d (u e) -> p d u e", u=2),
+                                    in0=v_sb[b][:, h, :].rearrange("p (e u d) -> p d u e", e=2, u=2),
                                     scalar1=1.0, scalar2=0.0, op0=ALU.mult, op1=ALU.add)
 
         def v_of(tiles, g):
@@ -276,14 +278,18 @@ def tile_parallelretention_fast3_pa_t_kernel(tc, q_scaled, k, v, omask, out):
         def store(g):
             b, h = HEADS[GROUP * g]
             for i in range(2):
-                nc.sync.dma_start(out=out[b + i, h:h + 2].rearrange("h (c p) d -> p (h c) d", p=P),
-                                  in_=o_sb[g, i][:].rearrange("p h c d -> p (h c) d"))
+                rows = out[b + i, h:h + 2].rearrange("h (c r m) d -> m r (h c) d", r=64, m=2)
+                for m in range(2):
+                    nc.sync.dma_start(out=rows[m],
+                                      in_=o_sb[g, i][64 * m:64 * m + 64].rearrange("p h c d -> p (h c) d"))
 
         def store_part(g, c0):
             for j in range(GROUP):
                 b, h = HEADS[GROUP * g + j]
-                nc.sync.dma_start(out=out[b, h].rearrange("(c p) d -> p c d", p=P)[:, c0:c0 + 2, :],
-                                  in_=o_sb[g, j % 2][:, j // 2, c0:c0 + 2, :])
+                rows = out[b, h].rearrange("(c r m) d -> m r c d", r=64, m=2)
+                for m in range(2):
+                    nc.sync.dma_start(out=rows[m, :, c0:c0 + 2, :],
+                                      in_=o_sb[g, j % 2][64 * m:64 * m + 64, j // 2, c0:c0 + 2, :])
 
         for h in range(H):
             for b in range(2):

@@ -108,7 +108,7 @@ def tile_parallelretention_fast3_pa_t_kernel(tc, q_scaled, k, v, omask, out):
         qkT, sc_c, sc_d = {}, {}, {}
         gab, gc0, gc1d = {}, {}, {}
         codes, scales, codes0, scales0, codes1, scales1 = {}, {}, {}, {}, {}, {}
-        rs, rp, vg, o_sb, qk_ps = {}, {}, {}, {}, {}
+        rs, rp, vg, o_sb, qk_ps, low_ps, sc_ps = {}, {}, {}, {}, {}, {}, {}
 
         def t_qk(n, part):
             b, h = HEADS[n]
@@ -128,19 +128,36 @@ def tile_parallelretention_fast3_pa_t_kernel(tc, q_scaled, k, v, omask, out):
                 qkT[n] = work.tile([P, 2 * S], BF16, name="qkT")
                 nc.scalar.copy(out=qkT[n][:].bitcast(F32), in_=qk_ps[n][:].bitcast(F32))
 
-        def score(n, c):
+        def score(n, chunks):
+            for c in chunks:
+                score_mm(n, c)
+            for c in chunks:
+                score_mask(n, c)
+
+        def score_mm(n, c):
             g, j = divmod(n, GROUP)
-            h = HEADS[n][1]
             if g not in rs:
                 rs[g] = work.tile([P, 4 * GROUP], F32, name="rs")
                 sc_c[g] = work.tile([P, 2, 2, 2 * P], BF16, name="sc_c", bufs=2)
                 sc_d[g] = work.tile([P, 2, 2 * P], BF16, name="sc_d", bufs=2)
-            s_ps = psum.tile([P, S], F32, name="s_ps", bufs=3)
             half = 64 * (c + 1)
-            sc = s_ps[:, 0:2 * half].rearrange("q (u x) -> q u x", u=2)
+            if c > 1 or n not in low_ps:
+                s_ps = psum.tile([P, S], F32, name="s_ps", bufs=4)
+                if c <= 1:
+                    low_ps[n] = s_ps
+            else:
+                s_ps = low_ps[n]
+            at = 256 if c == 0 else 0
+            sc = s_ps[:, at:at + 2 * half].rearrange("q (u x) -> q u x", u=2)
             nc.tensor.matmul(out=sc, lhsT=qkT[n][:, S + c * P:S + (c + 1) * P],
                              rhs=qkT[n][:, 0:S].rearrange("d (u x) -> d u x", u=2)[:, :, 0:half],
                              start=True, stop=True)
+            sc_ps[n, c] = sc
+
+        def score_mask(n, c):
+            g, j = divmod(n, GROUP)
+            h = HEADS[n][1]
+            half = 64 * (c + 1)
             if c == 3:
                 dst = ab_tiles[n % 3][:, 0, :, :]
             elif c == 2:
@@ -150,7 +167,7 @@ def tile_parallelretention_fast3_pa_t_kernel(tc, q_scaled, k, v, omask, out):
             else:
                 dst = sc_d[g][:, :, j * half:(j + 1) * half]
             nc.vector.scalar_tensor_tensor(
-                out=dst, in0=sc, scalar=1.0,
+                out=dst, in0=sc_ps[n, c], scalar=1.0,
                 in1=om_sb[h][:, c, 0:2 * half].rearrange("q (u x) -> q u x", u=2),
                 op0=ALU.mult, op1=ALU.mult, accum_out=rs[g][:, 4 * j + c:4 * j + c + 1])
 
@@ -244,9 +261,16 @@ def tile_parallelretention_fast3_pa_t_kernel(tc, q_scaled, k, v, omask, out):
             else:
                 nc.scalar.activation(out=dst, in_=src, func=ACT.Copy, scale=factor)
 
-        def out_ab(n0, on_vector):
+        def out_bank(last_group):
+            if last_group:
+                bank = psum.tile([P, S], F32, name="s_ps", bufs=4)
+            else:
+                bank = psum.tile([P, S], F32, name="o_ps")
+            return bank
+
+        def out_ab(n0, on_vector, last_group=False):
             g = n0 // GROUP
-            o_ps = psum.tile([P, S], F32, name="o_ps", bufs=2)
+            o_ps = out_bank(last_group)
             parts = [(n0 + i // 2, 3 - i % 2) for i in range(4)]
             for i, (n, c) in enumerate(parts):
                 slot = slice((3 - c) * P, (4 - c) * P)
@@ -258,8 +282,8 @@ def tile_parallelretention_fast3_pa_t_kernel(tc, q_scaled, k, v, omask, out):
             for i, (n, c) in enumerate(parts):
                 scaled(n, c, o_ps[:, i * P:(i + 1) * P], on_vector)
 
-        def out_c(g, on_vector):
-            o_ps = psum.tile([P, S], F32, name="o_ps", bufs=2)
+        def out_c(g, on_vector, last_group=False):
+            o_ps = out_bank(last_group)
             for i, (lc, ls) in enumerate(((codes0[g], scales0[g]), (codes1[g], scales1[g]))):
                 mx(o_ps[:, i * 256:(i + 1) * 256], lc[:, 0:P], ls[:, 0:P],
                    packed(vc_codes, g)[:, 2 * i:2 * i + 2, :].rearrange("p h d -> p (h d)"),
@@ -267,8 +291,8 @@ def tile_parallelretention_fast3_pa_t_kernel(tc, q_scaled, k, v, omask, out):
             for j in range(GROUP):
                 scaled(GROUP * g + j, 1, o_ps[:, j * P:(j + 1) * P], on_vector)
 
-        def out_d(g, on_vector):
-            o_ps = psum.tile([P, S], F32, name="o_ps", bufs=2)
+        def out_d(g, on_vector, last_group=False):
+            o_ps = out_bank(last_group)
             mx(o_ps[:], codes1[g][:, P:2 * P], scales1[g][:, P:2 * P],
                packed(vd_codes, g).rearrange("p h d -> p (h d)"),
                packed(vd_scales, g).rearrange("p h d -> p (h d)"))
@@ -323,7 +347,7 @@ def tile_parallelretention_fast3_pa_t_kernel(tc, q_scaled, k, v, omask, out):
         for step in range(NH + 1):
             g, j = divmod(step, GROUP)
             live = step < NH
-            order = (0, 1, 2, 3) if step == 0 else (3, 2, 1, 0)
+            order = ((1, 0), (2,), (3,)) if step == 0 else ((3,), (2,), (1, 0))
             if live:
                 score(step, order[0])
             if step == 0:
@@ -344,8 +368,6 @@ def tile_parallelretention_fast3_pa_t_kernel(tc, q_scaled, k, v, omask, out):
                     store(g - 1)
             if live:
                 score(step, order[1])
-            if step + LAG_T < NH:
-                t_qk(step + LAG_T, 0)
             m = step - LAG_Q
             if 0 <= m < NH:
                 quant(codes, scales, m, gab, 2 * P, "ab", 6)
@@ -361,13 +383,12 @@ def tile_parallelretention_fast3_pa_t_kernel(tc, q_scaled, k, v, omask, out):
             if live:
                 score(step, order[2])
             if step + LAG_T < NH:
-                t_qk(step + LAG_T, 1)
+                for part in range(2):
+                    t_qk(step + LAG_T, part)
             if 0 <= last < NH and last % GROUP == 1:
                 t_c0(last // GROUP)
             if 0 <= last < NH and last % GROUP == 3:
                 t_c1d(last // GROUP)
-            if live:
-                score(step, order[3])
             if step + LAG_V < NH:
                 v_regroup(step + LAG_V)
             if step == 1:
@@ -386,11 +407,11 @@ def tile_parallelretention_fast3_pa_t_kernel(tc, q_scaled, k, v, omask, out):
                 load_part(pair + 2, part)
             if live and j == GROUP - 1:
                 p_ops(g)
-        out_ab(NH - 4, False)
+        out_ab(NH - 4, False, True)
         quant(codes, scales, NH - 1, gab, 2 * P, "ab", 6)
-        out_ab(NH - 2, True)
+        out_ab(NH - 2, True, True)
         store_part(NG - 1, 2)
         quant(codes1, scales1, NG - 1, gc1d, 2 * P, "c1d", 2)
-        out_c(NG - 1, False)
-        out_d(NG - 1, True)
+        out_c(NG - 1, False, True)
+        out_d(NG - 1, True, True)
         store_part(NG - 1, 0)

@@ -108,7 +108,7 @@ def tile_parallelretention_fast3_pa_t_kernel(tc, q_scaled, k, v, omask, out):
         qkT, sc_c, sc_d = {}, {}, {}
         gab, gc0, gc1d = {}, {}, {}
         codes, scales, codes0, scales0, codes1, scales1 = {}, {}, {}, {}, {}, {}
-        rs, rp, vg, o_sb, qk_ps, low_ps, sc_ps = {}, {}, {}, {}, {}, {}, {}
+        rs, rp, vg, o_sb, qk_ps, low_ps, sc_ps, ab = {}, {}, {}, {}, {}, {}, {}, {}
 
         def t_qk(n, part):
             b, h = HEADS[n]
@@ -178,34 +178,37 @@ def tile_parallelretention_fast3_pa_t_kernel(tc, q_scaled, k, v, omask, out):
                                     words[:, u * P:(u + 1) * P], ident_f[:])
 
         def x_out(dst, bank, nslots):
-            nc.scalar.copy(out=dst[:].bitcast(F32).rearrange("p (x u) -> p x u", u=2),
+            nc.scalar.copy(out=dst.bitcast(F32).rearrange("p (x u) -> p x u", u=2),
                            in_=bank[:, 0:nslots * 256].rearrange("p (u x) -> p x u", u=2))
 
         def t_ab(n):
             x_ab = psum.tile([P, S], F32, name="x_ps", bufs=2)
             for slot in range(2):
                 t_slot(x_ab, slot, 2, ab_tiles[n % 3][:, slot, :, :])
-            gab[n] = work.tile([P, 2 * S], BF16, name="gab", align_bytes=64)
-            x_out(gab[n], x_ab, 2)
+            if n % 2 == 0:
+                gab[n // 2] = work.tile([P, 4 * S], BF16, name="gab", bufs=2, align_bytes=64)
+            x_out(gab[n // 2][:, 2 * S * (n % 2):2 * S * (n % 2 + 1)], x_ab, 2)
 
         def t_c0(g):
             x_cd = psum.tile([P, S], F32, name="x_ps", bufs=2)
             t_slot(x_cd, 0, 1, sc_c[g][:, 0, :, :])
             gc0[g] = work.tile([P, S], BF16, name="gc0", bufs=2, align_bytes=64)
-            x_out(gc0[g], x_cd, 1)
+            x_out(gc0[g][:], x_cd, 1)
 
         def t_c1d(g):
             x_cd = psum.tile([P, S], F32, name="x_ps", bufs=2)
             t_slot(x_cd, 0, 2, sc_c[g][:, 1, :, :])
             t_slot(x_cd, 1, 2, sc_d[g][:])
             gc1d[g] = work.tile([P, 2 * S], BF16, name="gc1d", bufs=2, align_bytes=64)
-            x_out(gc1d[g], x_cd, 2)
+            x_out(gc1d[g][:], x_cd, 2)
 
-        def quant(dst_codes, dst_scales, key, src, width, nm, bufs):
-            dst_codes[key] = work.tile([P, width], U32, name="codes_" + nm, bufs=bufs, align_bytes=64)
-            dst_scales[key] = work.tile([P, width], U8, name="scales_" + nm, bufs=bufs, align_bytes=64)
-            nc.vector.quantize_mx(out=dst_codes[key][:].bitcast(FP8X4), scales=dst_scales[key][:],
-                                  in_=src[key][:])
+        def quant(dst_codes, dst_scales, key, src, width, nm, bufs, halves=(0, 1)):
+            if halves[0] == 0:
+                dst_codes[key] = work.tile([P, width // 4], U32, name="codes_" + nm, bufs=bufs, align_bytes=64)
+                dst_scales[key] = work.tile([P, width // 4], U8, name="scales_" + nm, bufs=bufs, align_bytes=64)
+            lo, hi = halves[0] * width // 2, (halves[-1] + 1) * width // 2
+            nc.vector.quantize_mx(out=dst_codes[key][:, lo // 4:hi // 4].bitcast(FP8X4),
+                                  scales=dst_scales[key][:, lo // 4:hi // 4], in_=src[key][:, lo:hi])
 
         def v_regroup(n):
             g, j = divmod(n, GROUP)
@@ -237,13 +240,16 @@ def tile_parallelretention_fast3_pa_t_kernel(tc, q_scaled, k, v, omask, out):
                 nc.sync.dma_start(out=d_codes[32 * j:32 * j + 32, j::GROUP, :], in_=vc[0:32, j::GROUP, :])
                 nc.sync.dma_start(out=d_scales[32 * j:32 * j + 4, j::GROUP, :], in_=vs[0:4, j::GROUP, :])
 
-        def p_ops(g):
-            ab = work.tile([P, 4 * GROUP], F32, name="ab")
-            rp[g] = work.tile([P, 4 * GROUP], F32, name="rp")
-            nc.vector.scalar_tensor_tensor(out=ab[:], in0=rs[g][:], scalar=-1.0, in1=rs[g][:],
-                                           op0=ALU.mult, op1=ALU.max)
-            nc.vector.tensor_scalar_max(out=ab[:], in0=ab[:], scalar1=1.0)
-            nc.vector.reciprocal(out=rp[g][:], in_=ab[:])
+        def p_ops(g, part):
+            if part == 0:
+                ab[g] = work.tile([P, 4 * GROUP], F32, name="ab")
+                nc.vector.scalar_tensor_tensor(out=ab[g][:], in0=rs[g][:], scalar=-1.0, in1=rs[g][:],
+                                               op0=ALU.mult, op1=ALU.max)
+            elif part == 1:
+                nc.vector.tensor_scalar_max(out=ab[g][:], in0=ab[g][:], scalar1=1.0)
+            else:
+                rp[g] = work.tile([P, 4 * GROUP], F32, name="rp")
+                nc.vector.reciprocal(out=rp[g][:], in_=ab[g][:])
 
         def packed(tiles, g):
             return tiles[g // 2 % 2][:, GROUP * (g % 2):GROUP * (g % 2 + 1), :]
@@ -273,8 +279,8 @@ def tile_parallelretention_fast3_pa_t_kernel(tc, q_scaled, k, v, omask, out):
             o_ps = out_bank(last_group)
             parts = [(n0 + i // 2, 3 - i % 2) for i in range(4)]
             for i, (n, c) in enumerate(parts):
-                slot = slice((3 - c) * P, (4 - c) * P)
-                mx(o_ps[:, i * P:(i + 1) * P], codes[n][:, slot], scales[n][:, slot],
+                slot = slice(i * P, (i + 1) * P)
+                mx(o_ps[:, slot], codes[n // 2][:, slot], scales[n // 2][:, slot],
                    v_of(vcodes, g)[:, n % GROUP, :], v_of(vscales, g)[:, n % GROUP, :])
             if n0 % GROUP == 0:
                 for i in range(2):
@@ -350,6 +356,8 @@ def tile_parallelretention_fast3_pa_t_kernel(tc, q_scaled, k, v, omask, out):
             order = ((1, 0), (2,), (3,)) if step == 0 else ((3,), (2,), (1, 0))
             if live:
                 score(step, order[0])
+            if j == 0 and g > 0:
+                p_ops(g - 1, 0)
             if step == 0:
                 for part in range(2):
                     t_qk(1, part)
@@ -368,13 +376,18 @@ def tile_parallelretention_fast3_pa_t_kernel(tc, q_scaled, k, v, omask, out):
                     store(g - 1)
             if live:
                 score(step, order[1])
+            if j == 0 and g > 0 and live:
+                p_ops(g - 1, 1)
             m = step - LAG_Q
             if 0 <= m < NH:
-                quant(codes, scales, m, gab, 2 * P, "ab", 6)
+                if m == NH - 2:
+                    quant(codes, scales, m // 2, gab, 4 * S, "ab", 3, (0,))
+                elif m % 2 == 1:
+                    quant(codes, scales, m // 2, gab, 4 * S, "ab", 3)
                 if m % GROUP == 1:
-                    quant(codes0, scales0, m // GROUP, gc0, P, "c0", 2)
+                    quant(codes0, scales0, m // GROUP, gc0, S, "c0", 2)
                 if m % GROUP == 3:
-                    quant(codes1, scales1, m // GROUP, gc1d, 2 * P, "c1d", 2)
+                    quant(codes1, scales1, m // GROUP, gc1d, 2 * S, "c1d", 2)
             last = step - LAG_X
             if 0 <= last < NH - 1:
                 t_ab(last)
@@ -382,6 +395,8 @@ def tile_parallelretention_fast3_pa_t_kernel(tc, q_scaled, k, v, omask, out):
                 t_ab(step)
             if live:
                 score(step, order[2])
+            if j == 0 and g > 0 and live:
+                p_ops(g - 1, 2)
             if step + LAG_T < NH:
                 for part in range(2):
                     t_qk(step + LAG_T, part)
@@ -405,13 +420,13 @@ def tile_parallelretention_fast3_pa_t_kernel(tc, q_scaled, k, v, omask, out):
             pair, part = divmod(step - 5, 8)
             if step >= 5 and part < 6 and pair + 2 < NP:
                 load_part(pair + 2, part)
-            if live and j == GROUP - 1:
-                p_ops(g)
+        p_ops(NG - 1, 1)
+        quant(codes, scales, NH // 2 - 1, gab, 4 * S, "ab", 3, (1,))
+        p_ops(NG - 1, 2)
         out_ab(NH - 4, False, True)
-        quant(codes, scales, NH - 1, gab, 2 * P, "ab", 6)
         out_ab(NH - 2, True, True)
         store_part(NG - 1, 2)
-        quant(codes1, scales1, NG - 1, gc1d, 2 * P, "c1d", 2)
+        quant(codes1, scales1, NG - 1, gc1d, 2 * S, "c1d", 2)
         out_c(NG - 1, False, True)
         out_d(NG - 1, True, True)
         store_part(NG - 1, 0)

@@ -123,7 +123,11 @@ def tile_parallelretention_fast3_pa_t_kernel(tc, q_scaled, k, v, omask, out):
                     dst = qk_ps[n][:, S + 256 * i:S + 256 * (i + 1)].rearrange(
                         "d (c m r) -> d m c r", c=2, m=2)[:, m, :, :]
                     src = q_sb[b]
-                nc.tensor.transpose(dst, src[:, 2 * h + i, m * D:(m + 1) * D], ident_b[:])
+                row = src[:, 2 * h + i, m * D:(m + 1) * D]
+                if idx < 6:
+                    nc.tensor.matmul(out=dst, lhsT=row, rhs=ident_b[:], start=True, stop=True)
+                else:
+                    nc.tensor.transpose(dst, row, ident_b[:])
             if part == 1:
                 qkT[n] = work.tile([P, 2 * S], BF16, name="qkT")
                 nc.scalar.copy(out=qkT[n][:].bitcast(F32), in_=qk_ps[n][:].bitcast(F32))
@@ -388,22 +392,22 @@ def tile_parallelretention_fast3_pa_t_kernel(tc, q_scaled, k, v, omask, out):
                     quant(codes0, scales0, m // GROUP, gc0, S, "c0", 2)
                 if m % GROUP == 3:
                     quant(codes1, scales1, m // GROUP, gc1d, 2 * S, "c1d", 2)
+            if live:
+                score(step, order[2])
+            if j == 0 and g > 0 and live:
+                p_ops(g - 1, 2)
             last = step - LAG_X
             if 0 <= last < NH - 1:
                 t_ab(last)
             if step == NH - 1:
                 t_ab(step)
-            if live:
-                score(step, order[2])
-            if j == 0 and g > 0 and live:
-                p_ops(g - 1, 2)
-            if step + LAG_T < NH:
-                for part in range(2):
-                    t_qk(step + LAG_T, part)
             if 0 <= last < NH and last % GROUP == 1:
                 t_c0(last // GROUP)
             if 0 <= last < NH and last % GROUP == 3:
                 t_c1d(last // GROUP)
+            if step + LAG_T < NH:
+                for part in range(2):
+                    t_qk(step + LAG_T, part)
             if step + LAG_V < NH:
                 v_regroup(step + LAG_V)
             if step == 1:

@@ -44,7 +44,7 @@ def tile_parallelretention_fast3_pa_t_kernel(tc, q_scaled, k, v, omask, out):
 
         q_sb, k_sb, v_sb, om_sb, vcodes, vscales = [], [], [], [], [], []
         for b in range(B):
-            q_sb.append(res.tile([P, H * 2, 2 * D], BF16, name="q_sb%d" % b))
+            q_sb.append(res.tile([P, H * 4, D], BF16, name="q_sb%d" % b))
             k_sb.append(res.tile([P, H * 2, 2 * D], BF16, name="k_sb%d" % b))
             v_sb.append(res.tile([P, H, 4 * D], BF16, name="v_sb%d" % b))
         for p in range(NP):
@@ -86,8 +86,8 @@ def tile_parallelretention_fast3_pa_t_kernel(tc, q_scaled, k, v, omask, out):
                               in_=k[b, h:h + nh].rearrange("h (i r m) d -> r (h i) (m d)", i=2, m=2))
 
         def load_q(b, h, nh):
-            nc.sync.dma_start(out=q_sb[b][:, 2 * h:2 * (h + nh), :],
-                              in_=q_scaled[b, h:h + nh].rearrange("h (i r m) d -> r (h i) (m d)", i=2, m=2))
+            nc.sync.dma_start(out=q_sb[b][:, 4 * h:4 * (h + nh), :],
+                              in_=q_scaled[b, h:h + nh].rearrange("h (c r) d -> r (h c) d", r=P))
 
         def load_v(b, h, nh):
             nc.sync.dma_start(out=v_sb[b][:, h:h + nh, :],
@@ -95,11 +95,10 @@ def tile_parallelretention_fast3_pa_t_kernel(tc, q_scaled, k, v, omask, out):
 
         def load_mask(h):
             om_raw[h] = work.tile([P, 4, S], BF16, name="om_raw", bufs=4)
-            rows = omask[0, h].rearrange("(c r m) j -> m r c j", r=64, m=2)
+            rows = omask[0, h].rearrange("(c r) j -> r c j", r=P)
             for i in range(2):
-                for m in range(2):
-                    nc.sync.dma_start(out=om_raw[h][64 * m:64 * m + 64, 2 * i:2 * i + 2, 0:256 * (i + 1)],
-                                      in_=rows[m, :, 2 * i:2 * i + 2, 0:256 * (i + 1)])
+                nc.sync.dma_start(out=om_raw[h][:, 2 * i:2 * i + 2, 0:256 * (i + 1)],
+                                  in_=rows[:, 2 * i:2 * i + 2, 0:256 * (i + 1)])
 
         def load_part(p, part):
             b = 2 * p + part % 2
@@ -115,15 +114,14 @@ def tile_parallelretention_fast3_pa_t_kernel(tc, q_scaled, k, v, omask, out):
             if part == 0:
                 qk_ps[n] = psum.tile([P, 2 * S], BF16, name="qk_ps")
             for idx in range(4 * part, 4 * part + 4):
-                i, m = divmod(idx % 4, 2)
                 if idx < 4:
+                    i, m = divmod(idx, 2)
                     dst = qk_ps[n][:, 256 * m + P * i:256 * m + P * (i + 1)]
-                    src = k_sb[b]
+                    row = k_sb[b][:, 2 * h + i, m * D:(m + 1) * D]
                 else:
-                    dst = qk_ps[n][:, S + 256 * i:S + 256 * (i + 1)].rearrange(
-                        "d (c m r) -> d m c r", c=2, m=2)[:, m, :, :]
-                    src = q_sb[b]
-                row = src[:, 2 * h + i, m * D:(m + 1) * D]
+                    c = idx - 4
+                    dst = qk_ps[n][:, S + P * c:S + P * (c + 1)]
+                    row = q_sb[b][:, 4 * h + c, :]
                 if idx < 6:
                     nc.tensor.matmul(out=dst, lhsT=row, rhs=ident_b[:], start=True, stop=True)
                 else:
@@ -312,18 +310,14 @@ def tile_parallelretention_fast3_pa_t_kernel(tc, q_scaled, k, v, omask, out):
         def store(g):
             b, h = HEADS[GROUP * g]
             for i in range(2):
-                rows = out[b + i, h:h + 2].rearrange("h (c r m) d -> m r (h c) d", r=64, m=2)
-                for m in range(2):
-                    nc.sync.dma_start(out=rows[m],
-                                      in_=o_sb[g, i][64 * m:64 * m + 64].rearrange("p h c d -> p (h c) d"))
+                nc.sync.dma_start(out=out[b + i, h:h + 2].rearrange("h (c r) d -> r (h c) d", r=P),
+                                  in_=o_sb[g, i][:].rearrange("p h c d -> p (h c) d"))
 
         def store_part(g, c0):
             for j in range(GROUP):
                 b, h = HEADS[GROUP * g + j]
-                rows = out[b, h].rearrange("(c r m) d -> m r c d", r=64, m=2)
-                for m in range(2):
-                    nc.sync.dma_start(out=rows[m, :, c0:c0 + 2, :],
-                                      in_=o_sb[g, j % 2][64 * m:64 * m + 64, j // 2, c0:c0 + 2, :])
+                nc.sync.dma_start(out=out[b, h].rearrange("(c r) d -> r c d", r=P)[:, c0:c0 + 2, :],
+                                  in_=o_sb[g, j % 2][:, j // 2, c0:c0 + 2, :])
 
         for h in range(H):
             for b in range(2):

@@ -19,6 +19,7 @@ FLOPS = NH * 2 * (2 * S * S * D)
 
 HEADS = [(2 * pair + i, h) for pair in range(B // 2) for h in range(H) for i in range(2)]
 GROUP = 4
+VW = D + D // 4
 NG = NH // GROUP
 NP = NG // 2
 
@@ -42,14 +43,13 @@ def tile_parallelretention_fast3_pa_t_kernel(tc, q_scaled, k, v, omask, out):
         ident_f = const.tile([P, P], F32, name="ident_f")
         make_identity(nc, ident_f[:])
 
-        q_sb, k_sb, v_sb, om_sb, vcodes, vscales = [], [], [], [], [], []
+        q_sb, k_sb, v_sb, om_sb, vq = [], [], [], [], []
         for b in range(B):
             q_sb.append(res.tile([P, H * 4, D], BF16, name="q_sb%d" % b))
             k_sb.append(res.tile([P, H * 2, 2 * D], BF16, name="k_sb%d" % b))
             v_sb.append(res.tile([P, H, 4 * D], BF16, name="v_sb%d" % b))
         for p in range(NP):
-            vcodes.append(res.tile([P, 2 * GROUP, D], U32, name="vcodes%d" % p, align_bytes=64))
-            vscales.append(res.tile([P, 2 * GROUP, D], U8, name="vscales%d" % p, align_bytes=64))
+            vq.append(res.tile([P, 2 * GROUP, VW], U32, name="vq%d" % p, align_bytes=64))
         for h in range(H):
             om_sb.append(res.tile([P, 4, S], BF16, name="om_sb%d" % h))
 
@@ -58,15 +58,10 @@ def tile_parallelretention_fast3_pa_t_kernel(tc, q_scaled, k, v, omask, out):
             t = res.tile([P, 2, 2, 2 * P], BF16, name="ab_tile%d" % i)
             nc.vector.memset(t[:, 1, :, 192:256], 0.0)
             ab_tiles.append(t)
-        vc_codes, vc_scales, vd_codes, vd_scales, zeroed = [], [], [], [], []
+        vc, vd = [], []
         for i in range(2):
-            for (cl, sl, nm) in ((vc_codes, vc_scales, "vc"), (vd_codes, vd_scales, "vd")):
-                t = res.tile([P, 2 * GROUP, D], U32, name="%s_codes%d" % (nm, i), align_bytes=64)
-                zeroed.append(t[:].bitcast(I32))
-                cl.append(t)
-                t2 = res.tile([P, 2 * GROUP, D], U8, name="%s_scales%d" % (nm, i), align_bytes=64)
-                zeroed.append(t2[:].rearrange("p h d -> p (h d)").bitcast(I32))
-                sl.append(t2)
+            vc.append(res.tile([P, 2 * GROUP, VW], U32, name="vc%d" % i, align_bytes=64))
+            vd.append(res.tile([P, 2 * GROUP, VW], U32, name="vd%d" % i, align_bytes=64))
 
         def order_mask(h):
             for c in range(4):
@@ -213,34 +208,30 @@ def tile_parallelretention_fast3_pa_t_kernel(tc, q_scaled, k, v, omask, out):
                                   scales=dst_scales[key][:, lo // 4:hi // 4], in_=src[key][:, lo:hi])
 
         def v_regroup(n):
-            g, j = divmod(n, GROUP)
             b, h = HEADS[n]
-            if j == 0:
-                vg[g] = work.tile([P, GROUP, D, 4], BF16, name="vg", bufs=2, align_bytes=64)
-            nc.gpsimd.tensor_scalar(out=vg[g][:, j, :, :].rearrange("p d (u e) -> p d u e", u=2),
+            vg[n] = work.tile([P, D, 4], BF16, name="vg", bufs=6, align_bytes=64)
+            nc.gpsimd.tensor_scalar(out=vg[n][:].rearrange("p d (u e) -> p d u e", u=2),
                                     in0=v_sb[b][:, h, :].rearrange("p (e u d) -> p d u e", e=2, u=2),
                                     scalar1=1.0, scalar2=0.0, op0=ALU.mult, op1=ALU.add)
 
-        def v_of(tiles, g):
-            return tiles[g // 2][:, GROUP * (g % 2):GROUP * (g % 2 + 1), :]
+        def v_codes(tiles, n):
+            return tiles[:, n % (2 * GROUP), 0:D]
 
-        def v_quant(g):
-            nc.vector.quantize_mx(out=v_of(vcodes, g).rearrange("p h d -> p (h d)").bitcast(FP8X4),
-                                  scales=v_of(vscales, g).rearrange("p h d -> p (h d)"),
-                                  in_=vg[g][:].rearrange("p h d t -> p (h d t)"))
+        def v_scales(tiles, n):
+            return tiles[:, n % (2 * GROUP), D:VW].bitcast(U8)
+
+        def v_quant(n):
+            t = vq[n // (2 * GROUP)]
+            nc.vector.quantize_mx(out=v_codes(t, n).bitcast(FP8X4), scales=v_scales(t, n),
+                                  in_=vg[n][:].rearrange("p d t -> p (d t)"))
 
         def v_move(p):
-            vc, vs = vcodes[p][:].bitcast(I32), vscales[p][:].bitcast(I32)
-            c_codes, c_scales = vc_codes[p % 2][:].bitcast(I32), vc_scales[p % 2][:].bitcast(I32)
-            d_codes, d_scales = vd_codes[p % 2][:].bitcast(I32), vd_scales[p % 2][:].bitcast(I32)
+            src = vq[p][:].bitcast(I32)
+            c_dst, d_dst = vc[p % 2][:].bitcast(I32), vd[p % 2][:].bitcast(I32)
             for i in range(2):
-                nc.sync.dma_start(out=c_codes[64 * i:64 * i + 64, i::2, :], in_=vc[0:64, i::2, :])
-                for r in (0, 32):
-                    nc.sync.dma_start(out=c_scales[64 * i + r:64 * i + r + 4, i::2, :],
-                                      in_=vs[r:r + 4, i::2, :])
+                nc.sync.dma_start(out=c_dst[64 * i:64 * i + 64, i::2, :], in_=src[0:64, i::2, :])
             for j in range(GROUP):
-                nc.sync.dma_start(out=d_codes[32 * j:32 * j + 32, j::GROUP, :], in_=vc[0:32, j::GROUP, :])
-                nc.sync.dma_start(out=d_scales[32 * j:32 * j + 4, j::GROUP, :], in_=vs[0:4, j::GROUP, :])
+                nc.sync.dma_start(out=d_dst[32 * j:32 * j + 32, j::GROUP, :], in_=src[0:32, j::GROUP, :])
 
         def p_ops(g, part):
             if part == 0:
@@ -253,12 +244,10 @@ def tile_parallelretention_fast3_pa_t_kernel(tc, q_scaled, k, v, omask, out):
                 rp[g] = work.tile([P, 4 * GROUP], F32, name="rp")
                 nc.vector.reciprocal(out=rp[g][:], in_=ab[g][:])
 
-        def packed(tiles, g):
-            return tiles[g // 2 % 2][:, GROUP * (g % 2):GROUP * (g % 2 + 1), :]
-
-        def mx(o, lc, ls, rc, rsc):
-            nc.tensor.matmul_mx(out=o, lhsT=lc.bitcast(FP8X4), lhsT_scale=ls, rhs=rc.bitcast(FP8X4),
-                                rhs_scale=rsc, start=True, stop=True)
+        def mx(o, lc, ls, tiles, n):
+            nc.tensor.matmul_mx(out=o, lhsT=lc.bitcast(FP8X4), lhsT_scale=ls,
+                                rhs=v_codes(tiles, n).bitcast(FP8X4), rhs_scale=v_scales(tiles, n),
+                                start=True, stop=True)
 
         def scaled(n, c, src, on_vector):
             g, j = divmod(n, GROUP)
@@ -282,8 +271,7 @@ def tile_parallelretention_fast3_pa_t_kernel(tc, q_scaled, k, v, omask, out):
             parts = [(n0 + i // 2, 3 - i % 2) for i in range(4)]
             for i, (n, c) in enumerate(parts):
                 slot = slice(i * P, (i + 1) * P)
-                mx(o_ps[:, slot], codes[n // 2][:, slot], scales[n // 2][:, slot],
-                   v_of(vcodes, g)[:, n % GROUP, :], v_of(vscales, g)[:, n % GROUP, :])
+                mx(o_ps[:, slot], codes[n // 2][:, slot], scales[n // 2][:, slot], vq[g // 2], n)
             if n0 % GROUP == 0:
                 for i in range(2):
                     o_sb[g, i] = work.tile([P, 2, 4, D], F32, name="o_sb", bufs=4)
@@ -292,18 +280,17 @@ def tile_parallelretention_fast3_pa_t_kernel(tc, q_scaled, k, v, omask, out):
 
         def out_c(g, on_vector, last_group=False):
             o_ps = out_bank(last_group)
-            for i, (lc, ls) in enumerate(((codes0[g], scales0[g]), (codes1[g], scales1[g]))):
-                mx(o_ps[:, i * 256:(i + 1) * 256], lc[:, 0:P], ls[:, 0:P],
-                   packed(vc_codes, g)[:, 2 * i:2 * i + 2, :].rearrange("p h d -> p (h d)"),
-                   packed(vc_scales, g)[:, 2 * i:2 * i + 2, :].rearrange("p h d -> p (h d)"))
+            for j in range(GROUP):
+                lc, ls = ((codes0[g], scales0[g]), (codes1[g], scales1[g]))[j // 2]
+                mx(o_ps[:, j * P:(j + 1) * P], lc[:, 0:P], ls[:, 0:P], vc[g // 2 % 2], GROUP * g + j)
             for j in range(GROUP):
                 scaled(GROUP * g + j, 1, o_ps[:, j * P:(j + 1) * P], on_vector)
 
         def out_d(g, on_vector, last_group=False):
             o_ps = out_bank(last_group)
-            mx(o_ps[:], codes1[g][:, P:2 * P], scales1[g][:, P:2 * P],
-               packed(vd_codes, g).rearrange("p h d -> p (h d)"),
-               packed(vd_scales, g).rearrange("p h d -> p (h d)"))
+            for j in range(GROUP):
+                mx(o_ps[:, j * P:(j + 1) * P], codes1[g][:, P:2 * P], scales1[g][:, P:2 * P],
+                   vd[g // 2 % 2], GROUP * g + j)
             for j in range(GROUP):
                 scaled(GROUP * g + j, 0, o_ps[:, j * P:(j + 1) * P], on_vector)
 
@@ -332,13 +319,15 @@ def tile_parallelretention_fast3_pa_t_kernel(tc, q_scaled, k, v, omask, out):
         for b in (2, 3):
             load_k(b, 0, 2)
             load_q(b, 0, 2)
-        for view in zeroed[4:8]:
-            nc.vector.memset(view, 0)
+        for t in vq[0:2]:
+            nc.vector.memset(t[:, :, D:VW].bitcast(I32), 0)
+        for t in (vc[1], vd[1]):
+            nc.vector.memset(t[:].bitcast(I32), 0)
         order_mask(0)
         for part in range(2):
             t_qk(0, part)
-        for view in zeroed[0:4]:
-            nc.gpsimd.memset(view, 0)
+        for t in (vc[0], vd[0]):
+            nc.gpsimd.memset(t[:].bitcast(I32), 0)
         v_regroup(0)
         v_regroup(1)
         order_mask(1)
@@ -406,11 +395,14 @@ def tile_parallelretention_fast3_pa_t_kernel(tc, q_scaled, k, v, omask, out):
                 v_regroup(step + LAG_V)
             if step == 1:
                 order_mask(3)
-            for gg, at in enumerate([2, 4] + [4 * gg - 2 for gg in range(2, NG)]):
-                if step == at:
-                    v_quant(gg)
-                    if gg % 2 == 1:
-                        v_move(gg // 2)
+            for n in range(NH):
+                if step == (n // 2 + 1 if n < 2 * GROUP else n - 3):
+                    v_quant(n)
+                    if n % (2 * GROUP) == 2 * GROUP - 1:
+                        v_move(n // (2 * GROUP))
+            if step == 6:
+                for t in vq[2:4]:
+                    nc.gpsimd.memset(t[:, :, D:VW].bitcast(I32), 0)
             if step == 4:
                 for b in (2, 3):
                     load_k(b, 2, 2)

@@ -117,10 +117,7 @@ def tile_parallelretention_fast3_pa_t_kernel(tc, q_scaled, k, v, omask, out):
                     c = idx - 4
                     dst = qk_ps[n][:, S + P * c:S + P * (c + 1)]
                     row = q_sb[b][:, 4 * h + c, :]
-                if idx < 6:
-                    nc.tensor.matmul(out=dst, lhsT=row, rhs=ident_b[:], start=True, stop=True)
-                else:
-                    nc.tensor.transpose(dst, row, ident_b[:])
+                nc.tensor.transpose(dst, row, ident_b[:])
             if part == 1:
                 qkT[n] = work.tile([P, 2 * S], BF16, name="qkT")
                 nc.scalar.copy(out=qkT[n][:].bitcast(F32), in_=qk_ps[n][:].bitcast(F32))

@@ -63,19 +63,6 @@ def tile_parallelretention_fast3_pa_t_kernel(tc, q_scaled, k, v, omask, out):
             vc.append(res.tile([P, 2 * GROUP, VW], U32, name="vc%d" % i, align_bytes=64))
             vd.append(res.tile([P, 2 * GROUP, VW], U32, name="vd%d" % i, align_bytes=64))
 
-        def order_mask(h):
-            for c in range(4):
-                keys = (c + 1) * P
-                dst = om_sb[h][:, c, 0:keys].rearrange("q (u p e) -> q u p e", u=2, e=2)
-                src = om_raw[h][:, c, 0:keys].rearrange("q (p e u) -> q u p e", u=2, e=2)
-                if h == 0:
-                    nc.vector.tensor_copy(out=dst, in_=src)
-                else:
-                    nc.gpsimd.tensor_scalar(out=dst, in0=src, scalar1=1.0, scalar2=0.0,
-                                            op0=ALU.mult, op1=ALU.add)
-
-        om_raw = {}
-
         def load_k(b, h, nh):
             nc.sync.dma_start(out=k_sb[b][:, 2 * h:2 * (h + nh), :],
                               in_=k[b, h:h + nh].rearrange("h (i r m) d -> r (h i) (m d)", i=2, m=2))
@@ -89,10 +76,9 @@ def tile_parallelretention_fast3_pa_t_kernel(tc, q_scaled, k, v, omask, out):
                               in_=v[b, h:h + nh].rearrange("h (p t) d -> p h (t d)", t=4))
 
         def load_mask(h):
-            om_raw[h] = work.tile([P, 4, S], BF16, name="om_raw", bufs=4)
             rows = omask[0, h].rearrange("(c r) j -> r c j", r=P)
             for i in range(2):
-                nc.sync.dma_start(out=om_raw[h][:, 2 * i:2 * i + 2, 0:256 * (i + 1)],
+                nc.sync.dma_start(out=om_sb[h][:, 2 * i:2 * i + 2, 0:256 * (i + 1)],
                                   in_=rows[:, 2 * i:2 * i + 2, 0:256 * (i + 1)])
 
         def load_part(p, part):
@@ -162,7 +148,7 @@ def tile_parallelretention_fast3_pa_t_kernel(tc, q_scaled, k, v, omask, out):
                 dst = sc_d[g][:, :, j * half:(j + 1) * half]
             nc.vector.scalar_tensor_tensor(
                 out=dst, in0=sc_ps[n, c], scalar=1.0,
-                in1=om_sb[h][:, c, 0:2 * half].rearrange("q (u x) -> q u x", u=2),
+                in1=om_sb[h][:, c, 0:2 * half].rearrange("q (x u) -> q u x", u=2),
                 op0=ALU.mult, op1=ALU.mult, accum_out=rs[g][:, 4 * j + c:4 * j + c + 1])
 
         def t_slot(bank, slot, nslots, src):
@@ -316,21 +302,16 @@ def tile_parallelretention_fast3_pa_t_kernel(tc, q_scaled, k, v, omask, out):
         for b in (2, 3):
             load_k(b, 0, 2)
             load_q(b, 0, 2)
-        for t in vq[0:2]:
+        for t in vq:
             nc.vector.memset(t[:, :, D:VW].bitcast(I32), 0)
-        for t in (vc[1], vd[1]):
+        for t in vc + vd:
             nc.vector.memset(t[:].bitcast(I32), 0)
-        order_mask(0)
         for part in range(2):
             t_qk(0, part)
-        for t in (vc[0], vd[0]):
-            nc.gpsimd.memset(t[:].bitcast(I32), 0)
         v_regroup(0)
         v_regroup(1)
-        order_mask(1)
         v_regroup(2)
         v_regroup(3)
-        order_mask(2)
         v_regroup(4)
         v_regroup(5)
 
@@ -342,9 +323,6 @@ def tile_parallelretention_fast3_pa_t_kernel(tc, q_scaled, k, v, omask, out):
                 score(step, order[0])
             if j == 0 and g > 0:
                 p_ops(g - 1, 0)
-            if step == 0:
-                for part in range(2):
-                    t_qk(1, part)
             if j == 0 and g > 1 and live:
                 out_d(g - 2, False)
             elif j == 1 and g > 0:
@@ -355,9 +333,6 @@ def tile_parallelretention_fast3_pa_t_kernel(tc, q_scaled, k, v, omask, out):
                 out_ab(step - 4, False)
             elif j == 3 and g > 0:
                 out_c(g - 1, False)
-                if step == NH - 1:
-                    out_d(g - 1, False)
-                    store(g - 1)
             if live:
                 score(step, order[1])
             if j == 0 and g > 0 and live:
@@ -380,26 +355,24 @@ def tile_parallelretention_fast3_pa_t_kernel(tc, q_scaled, k, v, omask, out):
             if 0 <= last < NH - 1:
                 t_ab(last)
             if step == NH - 1:
+                out_d(g - 1, False)
+                store(g - 1)
                 t_ab(step)
             if 0 <= last < NH and last % GROUP == 1:
                 t_c0(last // GROUP)
             if 0 <= last < NH and last % GROUP == 3:
                 t_c1d(last // GROUP)
-            if step + LAG_T < NH:
-                for part in range(2):
-                    t_qk(step + LAG_T, part)
+            for n in ((1, 2) if step == 0 else (step + LAG_T,)):
+                if n < NH:
+                    for part in range(2):
+                        t_qk(n, part)
             if step + LAG_V < NH:
                 v_regroup(step + LAG_V)
-            if step == 1:
-                order_mask(3)
             for n in range(NH):
                 if step == (n // 2 + 1 if n < 2 * GROUP else n - 3):
                     v_quant(n)
                     if n % (2 * GROUP) == 2 * GROUP - 1:
                         v_move(n // (2 * GROUP))
-            if step == 6:
-                for t in vq[2:4]:
-                    nc.gpsimd.memset(t[:, :, D:VW].bitcast(I32), 0)
             if step == 4:
                 for b in (2, 3):
                     load_k(b, 2, 2)
@@ -411,9 +384,9 @@ def tile_parallelretention_fast3_pa_t_kernel(tc, q_scaled, k, v, omask, out):
         quant(codes, scales, NH // 2 - 1, gab, 4 * S, "ab", 3, (1,))
         p_ops(NG - 1, 2)
         out_ab(NH - 4, False, True)
+        quant(codes1, scales1, NG - 1, gc1d, 2 * S, "c1d", 2)
         out_ab(NH - 2, True, True)
         store_part(NG - 1, 2)
-        quant(codes1, scales1, NG - 1, gc1d, 2 * S, "c1d", 2)
         out_c(NG - 1, False, True)
         out_d(NG - 1, True, True)
         store_part(NG - 1, 0)

@@ -111,7 +111,7 @@ def tile_parallelretention_fast3_pa_t_kernel(tc, q_scaled, k, v, omask, out):
         def score(n, chunks):
             for c in chunks:
                 score_mm(n, c)
-            for c in chunks:
+            for c in reversed(chunks):
                 score_mask(n, c)
 
         def score_mm(n, c):
@@ -157,9 +157,10 @@ def tile_parallelretention_fast3_pa_t_kernel(tc, q_scaled, k, v, omask, out):
                 nc.tensor.transpose(bank[:, (u * nslots + slot) * P:(u * nslots + slot + 1) * P],
                                     words[:, u * P:(u + 1) * P], ident_f[:])
 
-        def x_out(dst, bank, nslots):
-            nc.scalar.copy(out=dst.bitcast(F32).rearrange("p (x u) -> p x u", u=2),
-                           in_=bank[:, 0:nslots * 256].rearrange("p (u x) -> p x u", u=2))
+        def x_out(dst, bank, nslots, on_vector=False):
+            copy = nc.vector.tensor_copy if on_vector else nc.scalar.copy
+            copy(out=dst.bitcast(F32).rearrange("p (x u) -> p x u", u=2),
+                 in_=bank[:, 0:nslots * 256].rearrange("p (u x) -> p x u", u=2))
 
         def t_ab(n):
             x_ab = psum.tile([P, S], F32, name="x_ps", bufs=2)
@@ -180,7 +181,7 @@ def tile_parallelretention_fast3_pa_t_kernel(tc, q_scaled, k, v, omask, out):
             t_slot(x_cd, 0, 2, sc_c[g][:, 1, :, :])
             t_slot(x_cd, 1, 2, sc_d[g][:])
             gc1d[g] = work.tile([P, 2 * S], BF16, name="gc1d", bufs=2, align_bytes=64)
-            x_out(gc1d[g][:], x_cd, 2)
+            x_out(gc1d[g][:], x_cd, 2, on_vector=g == NG - 1)
 
         def quant(dst_codes, dst_scales, key, src, width, nm, bufs, halves=(0, 1)):
             if halves[0] == 0:
@@ -216,16 +217,18 @@ def tile_parallelretention_fast3_pa_t_kernel(tc, q_scaled, k, v, omask, out):
             for j in range(GROUP):
                 nc.sync.dma_start(out=d_dst[32 * j:32 * j + 32, j::GROUP, :], in_=src[0:32, j::GROUP, :])
 
-        def p_ops(g, part):
-            if part == 0:
+        def p_ops(g, part, heads=(0, GROUP)):
+            cols = slice(4 * heads[0], 4 * heads[1])
+            if g not in ab:
                 ab[g] = work.tile([P, 4 * GROUP], F32, name="ab")
-                nc.vector.scalar_tensor_tensor(out=ab[g][:], in0=rs[g][:], scalar=-1.0, in1=rs[g][:],
-                                               op0=ALU.mult, op1=ALU.max)
-            elif part == 1:
-                nc.vector.tensor_scalar_max(out=ab[g][:], in0=ab[g][:], scalar1=1.0)
-            else:
                 rp[g] = work.tile([P, 4 * GROUP], F32, name="rp")
-                nc.vector.reciprocal(out=rp[g][:], in_=ab[g][:])
+            if part == 0:
+                nc.vector.scalar_tensor_tensor(out=ab[g][:, cols], in0=rs[g][:, cols], scalar=-1.0,
+                                               in1=rs[g][:, cols], op0=ALU.mult, op1=ALU.max)
+            elif part == 1:
+                nc.vector.tensor_scalar_max(out=ab[g][:, cols], in0=ab[g][:, cols], scalar1=1.0)
+            else:
+                nc.vector.reciprocal(out=rp[g][:, cols], in_=ab[g][:, cols])
 
         def mx(o, lc, ls, tiles, n):
             nc.tensor.matmul_mx(out=o, lhsT=lc.bitcast(FP8X4), lhsT_scale=ls,
@@ -283,8 +286,14 @@ def tile_parallelretention_fast3_pa_t_kernel(tc, q_scaled, k, v, omask, out):
                 nc.sync.dma_start(out=out[b + i, h:h + 2].rearrange("h (c r) d -> r (h c) d", r=P),
                                   in_=o_sb[g, i][:].rearrange("p h c d -> p (h c) d"))
 
-        def store_part(g, c0):
-            for j in range(GROUP):
+        def store_chunk(g, c):
+            b, h = HEADS[GROUP * g]
+            for i in range(2):
+                nc.sync.dma_start(out=out[b + i, h:h + 2].rearrange("h (c r) d -> r h c d", r=P)[:, :, c, :],
+                                  in_=o_sb[g, i][:, :, c, :])
+
+        def store_part(g, c0, heads=range(GROUP)):
+            for j in heads:
                 b, h = HEADS[GROUP * g + j]
                 nc.sync.dma_start(out=out[b, h].rearrange("(c r) d -> r c d", r=P)[:, c0:c0 + 2, :],
                                   in_=o_sb[g, j % 2][:, j // 2, c0:c0 + 2, :])
@@ -318,11 +327,13 @@ def tile_parallelretention_fast3_pa_t_kernel(tc, q_scaled, k, v, omask, out):
         for step in range(NH + 1):
             g, j = divmod(step, GROUP)
             live = step < NH
-            order = ((1, 0), (2,), (3,)) if step == 0 else ((3,), (2,), (1, 0))
+            order = ((0, 1), (3, 2)) if step == 0 else ((2, 3), (0, 1))
             if live:
                 score(step, order[0])
-            if j == 0 and g > 0:
+            if j == 0 and 0 < g < NG:
                 p_ops(g - 1, 0)
+            if step == NH - 2:
+                p_ops(g, 0, (0, 2))
             if j == 0 and g > 1 and live:
                 out_d(g - 2, False)
             elif j == 1 and g > 0:
@@ -331,12 +342,14 @@ def tile_parallelretention_fast3_pa_t_kernel(tc, q_scaled, k, v, omask, out):
                     store(g - 2)
             elif j == 2 and g > 0:
                 out_ab(step - 4, False)
+                if g == NG - 1:
+                    store_part(g - 1, 2)
             elif j == 3 and g > 0:
                 out_c(g - 1, False)
-            if live:
-                score(step, order[1])
             if j == 0 and g > 0 and live:
                 p_ops(g - 1, 1)
+            if step == NH - 2:
+                p_ops(g, 1, (0, 2))
             m = step - LAG_Q
             if 0 <= m < NH:
                 if m == NH - 2:
@@ -348,16 +361,20 @@ def tile_parallelretention_fast3_pa_t_kernel(tc, q_scaled, k, v, omask, out):
                 if m % GROUP == 3:
                     quant(codes1, scales1, m // GROUP, gc1d, 2 * S, "c1d", 2)
             if live:
-                score(step, order[2])
+                score(step, order[1])
             if j == 0 and g > 0 and live:
                 p_ops(g - 1, 2)
+            if step == NH - 2:
+                p_ops(g, 2, (0, 2))
             last = step - LAG_X
             if 0 <= last < NH - 1:
                 t_ab(last)
             if step == NH - 1:
-                out_d(g - 1, False)
-                store(g - 1)
                 t_ab(step)
+                out_d(g - 1, False)
+                store_part(g - 1, 0)
+                out_ab(NH - 4, False, True)
+                store_part(g, 2, (0, 1))
             if 0 <= last < NH and last % GROUP == 1:
                 t_c0(last // GROUP)
             if 0 <= last < NH and last % GROUP == 3:
@@ -380,13 +397,14 @@ def tile_parallelretention_fast3_pa_t_kernel(tc, q_scaled, k, v, omask, out):
             pair, part = divmod(step - 5, 8)
             if step >= 5 and part < 6 and pair + 2 < NP:
                 load_part(pair + 2, part)
-        p_ops(NG - 1, 1)
+        p_ops(NG - 1, 0, (2, GROUP))
         quant(codes, scales, NH // 2 - 1, gab, 4 * S, "ab", 3, (1,))
-        p_ops(NG - 1, 2)
-        out_ab(NH - 4, False, True)
+        p_ops(NG - 1, 1, (2, GROUP))
         quant(codes1, scales1, NG - 1, gc1d, 2 * S, "c1d", 2)
-        out_ab(NH - 2, True, True)
-        store_part(NG - 1, 2)
-        out_c(NG - 1, False, True)
+        p_ops(NG - 1, 2, (2, GROUP))
+        out_ab(NH - 2, False, True)
+        store_part(NG - 1, 2, (2, 3))
+        out_c(NG - 1, True, True)
+        store_chunk(NG - 1, 1)
         out_d(NG - 1, True, True)
-        store_part(NG - 1, 0)
+        store_chunk(NG - 1, 0)

@@ -328,12 +328,12 @@ def tile_parallelretention_fast3_pa_t_kernel(tc, q_scaled, k, v, omask, out):
             g, j = divmod(step, GROUP)
             live = step < NH
             order = ((0, 1), (3, 2)) if step == 0 else ((2, 3), (0, 1))
-            if live:
-                score(step, order[0])
             if j == 0 and 0 < g < NG:
                 p_ops(g - 1, 0)
             if step == NH - 2:
                 p_ops(g, 0, (0, 2))
+            if live:
+                score(step, order[0])
             if j == 0 and g > 1 and live:
                 out_d(g - 2, False)
             elif j == 1 and g > 0:
@@ -352,14 +352,14 @@ def tile_parallelretention_fast3_pa_t_kernel(tc, q_scaled, k, v, omask, out):
                 p_ops(g, 1, (0, 2))
             m = step - LAG_Q
             if 0 <= m < NH:
-                if m == NH - 2:
-                    quant(codes, scales, m // 2, gab, 4 * S, "ab", 3, (0,))
-                elif m % 2 == 1:
-                    quant(codes, scales, m // 2, gab, 4 * S, "ab", 3)
                 if m % GROUP == 1:
                     quant(codes0, scales0, m // GROUP, gc0, S, "c0", 2)
                 if m % GROUP == 3:
                     quant(codes1, scales1, m // GROUP, gc1d, 2 * S, "c1d", 2)
+                if m == NH - 2:
+                    quant(codes, scales, m // 2, gab, 4 * S, "ab", 3, (0,))
+                elif m % 2 == 1:
+                    quant(codes, scales, m // 2, gab, 4 * S, "ab", 3)
             if live:
                 score(step, order[1])
             if j == 0 and g > 0 and live:

@@ -23,7 +23,8 @@ VW = D + D // 4
 NG = NH // GROUP
 NP = NG // 2
 
-LAG_T = 2
+BANKS = 4
+LAG_T = 3
 LAG_V = 6
 LAG_X = 1
 LAG_Q = 2
@@ -88,7 +89,8 @@ def tile_parallelretention_fast3_pa_t_kernel(tc, q_scaled, k, v, omask, out):
         qkT, sc_c, sc_d = {}, {}, {}
         gab, gc0, gc1d = {}, {}, {}
         codes, scales, codes0, scales0, codes1, scales1 = {}, {}, {}, {}, {}, {}
-        rs, rp, vg, o_sb, qk_ps, low_ps, sc_ps, ab = {}, {}, {}, {}, {}, {}, {}, {}
+        rs, rp, vg, o_sb, qk_ps, sc_ps, bank_of, ab = {}, {}, {}, {}, {}, {}, {}, {}
+        free_banks = list(range(BANKS))
 
         def t_qk(n, part):
             b, h = HEADS[n]
@@ -105,37 +107,33 @@ def tile_parallelretention_fast3_pa_t_kernel(tc, q_scaled, k, v, omask, out):
                     row = q_sb[b][:, 4 * h + c, :]
                 nc.tensor.transpose(dst, row, ident_b[:])
             if part == 1:
-                qkT[n] = work.tile([P, 2 * S], BF16, name="qkT")
+                qkT[n] = work.tile([P, 2 * S], BF16, name="qkT", bufs=4)
                 nc.scalar.copy(out=qkT[n][:].bitcast(F32), in_=qk_ps[n][:].bitcast(F32))
 
-        def score(n, chunks):
+        def score_mm(n, chunks):
+            bank = free_banks.pop(0)
+            s_ps = psum.tile([P, S], F32, name="s_ps%d" % bank)
             for c in chunks:
-                score_mm(n, c)
-            for c in reversed(chunks):
-                score_mask(n, c)
+                half = 64 * (c + 1)
+                at = 256 if c == 0 else 0
+                sc = s_ps[:, at:at + 2 * half].rearrange("q (u x) -> q u x", u=2)
+                nc.tensor.matmul(out=sc, lhsT=qkT[n][:, S + c * P:S + (c + 1) * P],
+                                 rhs=qkT[n][:, 0:S].rearrange("d (u x) -> d u x", u=2)[:, :, 0:half],
+                                 start=True, stop=True)
+                sc_ps[n, c] = sc
+            bank_of[n, chunks] = bank
 
-        def score_mm(n, c):
+        def score_mask(n, chunks):
+            for c in reversed(chunks):
+                mask_product(n, c)
+            free_banks.append(bank_of[n, chunks])
+
+        def mask_product(n, c):
             g, j = divmod(n, GROUP)
             if g not in rs:
                 rs[g] = work.tile([P, 4 * GROUP], F32, name="rs")
                 sc_c[g] = work.tile([P, 2, 2, 2 * P], BF16, name="sc_c", bufs=2)
                 sc_d[g] = work.tile([P, 2, 2 * P], BF16, name="sc_d", bufs=2)
-            half = 64 * (c + 1)
-            if c > 1 or n not in low_ps:
-                s_ps = psum.tile([P, S], F32, name="s_ps", bufs=4)
-                if c <= 1:
-                    low_ps[n] = s_ps
-            else:
-                s_ps = low_ps[n]
-            at = 256 if c == 0 else 0
-            sc = s_ps[:, at:at + 2 * half].rearrange("q (u x) -> q u x", u=2)
-            nc.tensor.matmul(out=sc, lhsT=qkT[n][:, S + c * P:S + (c + 1) * P],
-                             rhs=qkT[n][:, 0:S].rearrange("d (u x) -> d u x", u=2)[:, :, 0:half],
-                             start=True, stop=True)
-            sc_ps[n, c] = sc
-
-        def score_mask(n, c):
-            g, j = divmod(n, GROUP)
             h = HEADS[n][1]
             half = 64 * (c + 1)
             if c == 3:
@@ -193,7 +191,7 @@ def tile_parallelretention_fast3_pa_t_kernel(tc, q_scaled, k, v, omask, out):
 
         def v_regroup(n):
             b, h = HEADS[n]
-            vg[n] = work.tile([P, D, 4], BF16, name="vg", bufs=6, align_bytes=64)
+            vg[n] = work.tile([P, D, 4], BF16, name="vg", bufs=2, align_bytes=64)
             nc.gpsimd.tensor_scalar(out=vg[n][:].rearrange("p d (u e) -> p d u e", u=2),
                                     in0=v_sb[b][:, h, :].rearrange("p (e u d) -> p d u e", e=2, u=2),
                                     scalar1=1.0, scalar2=0.0, op0=ALU.mult, op1=ALU.add)
@@ -230,6 +228,13 @@ def tile_parallelretention_fast3_pa_t_kernel(tc, q_scaled, k, v, omask, out):
             else:
                 nc.vector.reciprocal(out=rp[g][:, cols], in_=ab[g][:, cols])
 
+        def p_part(step, part):
+            g, j = divmod(step, GROUP)
+            if j == 0 and 0 < g < NG:
+                p_ops(g - 1, part)
+            if step == NH - 2:
+                p_ops(g, part, (0, 2))
+
         def mx(o, lc, ls, tiles, n):
             nc.tensor.matmul_mx(out=o, lhsT=lc.bitcast(FP8X4), lhsT_scale=ls,
                                 rhs=v_codes(tiles, n).bitcast(FP8X4), rhs_scale=v_scales(tiles, n),
@@ -246,7 +251,9 @@ def tile_parallelretention_fast3_pa_t_kernel(tc, q_scaled, k, v, omask, out):
 
         def out_bank(last_group):
             if last_group:
-                bank = psum.tile([P, S], F32, name="s_ps", bufs=4)
+                k = free_banks.pop(0)
+                free_banks.append(k)
+                bank = psum.tile([P, S], F32, name="s_ps%d" % k)
             else:
                 bank = psum.tile([P, S], F32, name="o_ps")
             return bank
@@ -302,10 +309,12 @@ def tile_parallelretention_fast3_pa_t_kernel(tc, q_scaled, k, v, omask, out):
             for b in range(2):
                 load_k(b, h, 1)
                 load_q(b, h, 1)
-                if b == 0:
+                if b == 0 and h < 2:
                     load_mask(h)
             for b in range(2):
                 load_v(b, h, 1)
+            if h >= 2:
+                load_mask(h)
         for b in (2, 3):
             load_v(b, 0, H)
         for b in (2, 3):
@@ -317,23 +326,20 @@ def tile_parallelretention_fast3_pa_t_kernel(tc, q_scaled, k, v, omask, out):
             nc.vector.memset(t[:].bitcast(I32), 0)
         for part in range(2):
             t_qk(0, part)
-        v_regroup(0)
-        v_regroup(1)
-        v_regroup(2)
-        v_regroup(3)
-        v_regroup(4)
-        v_regroup(5)
+        for chunks in ((0, 1), (2,), (3,)):
+            score_mm(0, chunks)
+        for part in range(2):
+            t_qk(1, part)
+        for n in range(6):
+            v_regroup(n)
 
         for step in range(NH + 1):
             g, j = divmod(step, GROUP)
-            live = step < NH
-            order = ((0, 1), (3, 2)) if step == 0 else ((2, 3), (0, 1))
-            if j == 0 and 0 < g < NG:
-                p_ops(g - 1, 0)
-            if step == NH - 2:
-                p_ops(g, 0, (0, 2))
+            live, ahead = step < NH, step + 1 < NH
+            order = ((0, 1), (2,), (3,)) if step == 0 else ((3,), (2,), (0, 1))
+            p_part(step, 0)
             if live:
-                score(step, order[0])
+                score_mask(step, order[0])
             if j == 0 and g > 1 and live:
                 out_d(g - 2, False)
             elif j == 1 and g > 0:
@@ -346,10 +352,24 @@ def tile_parallelretention_fast3_pa_t_kernel(tc, q_scaled, k, v, omask, out):
                     store_part(g - 1, 2)
             elif j == 3 and g > 0:
                 out_c(g - 1, False)
-            if j == 0 and g > 0 and live:
-                p_ops(g - 1, 1)
-            if step == NH - 2:
-                p_ops(g, 1, (0, 2))
+            last = step - LAG_X
+            if 0 <= last < NH - 1:
+                t_ab(last)
+            if 0 <= last < NH - 1 and last % GROUP == 1:
+                t_c0(last // GROUP)
+            if 0 <= last < NH - 1 and last % GROUP == 3:
+                t_c1d(last // GROUP)
+            if step == 2:
+                for part in range(2):
+                    t_qk(step + LAG_T - 1, part)
+            if ahead:
+                score_mm(step + 1, (0, 1))
+                score_mm(step + 1, (2,))
+            if live:
+                score_mask(step, order[1])
+            if ahead:
+                score_mm(step + 1, (3,))
+            p_part(step, 1)
             m = step - LAG_Q
             if 0 <= m < NH:
                 if m % GROUP == 1:
@@ -360,29 +380,21 @@ def tile_parallelretention_fast3_pa_t_kernel(tc, q_scaled, k, v, omask, out):
                     quant(codes, scales, m // 2, gab, 4 * S, "ab", 3, (0,))
                 elif m % 2 == 1:
                     quant(codes, scales, m // 2, gab, 4 * S, "ab", 3)
+            n = step + (LAG_T if step >= 2 else LAG_T - 1)
+            if n < NH:
+                for part in range(2):
+                    t_qk(n, part)
             if live:
-                score(step, order[1])
-            if j == 0 and g > 0 and live:
-                p_ops(g - 1, 2)
-            if step == NH - 2:
-                p_ops(g, 2, (0, 2))
-            last = step - LAG_X
-            if 0 <= last < NH - 1:
-                t_ab(last)
+                score_mask(step, order[2])
+            p_part(step, 2)
             if step == NH - 1:
                 t_ab(step)
                 out_d(g - 1, False)
                 store_part(g - 1, 0)
                 out_ab(NH - 4, False, True)
                 store_part(g, 2, (0, 1))
-            if 0 <= last < NH and last % GROUP == 1:
-                t_c0(last // GROUP)
-            if 0 <= last < NH and last % GROUP == 3:
-                t_c1d(last // GROUP)
-            for n in ((1, 2) if step == 0 else (step + LAG_T,)):
-                if n < NH:
-                    for part in range(2):
-                        t_qk(n, part)
+            if step == NH:
+                t_c1d(g - 1)
             if step + LAG_V < NH:
                 v_regroup(step + LAG_V)
             for n in range(NH):

@@ -54,11 +54,14 @@ def tile_parallelretention_fast3_pa_t_kernel(tc, q_scaled, k, v, omask, out):
         for h in range(H):
             om_sb.append(res.tile([P, 4, S], BF16, name="om_sb%d" % h))
 
-        ab_tiles = []
+        ab_tiles, rs_tiles = [], []
         for i in range(3):
             t = res.tile([P, 2, 2, 2 * P], BF16, name="ab_tile%d" % i)
             nc.vector.memset(t[:, 1, :, 192:256], 0.0)
             ab_tiles.append(t)
+            t = res.tile([P, 4 * GROUP, 2], F32, name="rs_tile%d" % i)
+            nc.vector.memset(t[:], 1.0)
+            rs_tiles.append(t)
         vc, vd = [], []
         for i in range(2):
             vc.append(res.tile([P, 2 * GROUP, VW], U32, name="vc%d" % i, align_bytes=64))
@@ -89,7 +92,7 @@ def tile_parallelretention_fast3_pa_t_kernel(tc, q_scaled, k, v, omask, out):
         qkT, sc_c, sc_d = {}, {}, {}
         gab, gc0, gc1d = {}, {}, {}
         codes, scales, codes0, scales0, codes1, scales1 = {}, {}, {}, {}, {}, {}
-        rs, rp, vg, o_sb, qk_ps, sc_ps, bank_of, ab = {}, {}, {}, {}, {}, {}, {}, {}
+        rp, p_max, vg, o_sb, qk_ps, sc_ps, bank_of = {}, {}, {}, {}, {}, {}, {}
         free_banks = list(range(BANKS))
 
         def t_qk(n, part):
@@ -130,8 +133,7 @@ def tile_parallelretention_fast3_pa_t_kernel(tc, q_scaled, k, v, omask, out):
 
         def mask_product(n, c):
             g, j = divmod(n, GROUP)
-            if g not in rs:
-                rs[g] = work.tile([P, 4 * GROUP], F32, name="rs")
+            if g not in sc_c:
                 sc_c[g] = work.tile([P, 2, 2, 2 * P], BF16, name="sc_c", bufs=2)
                 sc_d[g] = work.tile([P, 2, 2 * P], BF16, name="sc_d", bufs=2)
             h = HEADS[n][1]
@@ -147,7 +149,7 @@ def tile_parallelretention_fast3_pa_t_kernel(tc, q_scaled, k, v, omask, out):
             nc.vector.scalar_tensor_tensor(
                 out=dst, in0=sc_ps[n, c], scalar=1.0,
                 in1=om_sb[h][:, c, 0:2 * half].rearrange("q (x u) -> q u x", u=2),
-                op0=ALU.mult, op1=ALU.mult, accum_out=rs[g][:, 4 * j + c:4 * j + c + 1])
+                op0=ALU.mult, op1=ALU.mult, accum_out=rs_tiles[g % 3][:, 4 * j + c, 0:1])
 
         def t_slot(bank, slot, nslots, src):
             words = src.rearrange("q u x -> q (u x)").bitcast(F32)
@@ -217,16 +219,14 @@ def tile_parallelretention_fast3_pa_t_kernel(tc, q_scaled, k, v, omask, out):
 
         def p_ops(g, part, heads=(0, GROUP)):
             cols = slice(4 * heads[0], 4 * heads[1])
-            if g not in ab:
-                ab[g] = work.tile([P, 4 * GROUP], F32, name="ab")
+            if g not in rp:
+                p_max[g] = work.tile([P, 4 * GROUP], F32, name="p_max")
                 rp[g] = work.tile([P, 4 * GROUP], F32, name="rp")
             if part == 0:
-                nc.vector.scalar_tensor_tensor(out=ab[g][:, cols], in0=rs[g][:, cols], scalar=-1.0,
-                                               in1=rs[g][:, cols], op0=ALU.mult, op1=ALU.max)
-            elif part == 1:
-                nc.vector.tensor_scalar_max(out=ab[g][:, cols], in0=ab[g][:, cols], scalar1=1.0)
+                nc.vector.tensor_reduce(out=p_max[g][:, cols], in_=rs_tiles[g % 3][:, cols, :], op=ALU.max,
+                                        axis=mybir.AxisListType.X, apply_absolute_value=True)
             else:
-                nc.vector.reciprocal(out=rp[g][:, cols], in_=ab[g][:, cols])
+                nc.vector.reciprocal(out=rp[g][:, cols], in_=p_max[g][:, cols])
 
         def p_part(step, part):
             g, j = divmod(step, GROUP)
@@ -386,7 +386,6 @@ def tile_parallelretention_fast3_pa_t_kernel(tc, q_scaled, k, v, omask, out):
                     t_qk(n, part)
             if live:
                 score_mask(step, order[2])
-            p_part(step, 2)
             if step == NH - 1:
                 t_ab(step)
                 out_d(g - 1, False)
@@ -413,7 +412,6 @@ def tile_parallelretention_fast3_pa_t_kernel(tc, q_scaled, k, v, omask, out):
         quant(codes, scales, NH // 2 - 1, gab, 4 * S, "ab", 3, (1,))
         p_ops(NG - 1, 1, (2, GROUP))
         quant(codes1, scales1, NG - 1, gc1d, 2 * S, "c1d", 2)
-        p_ops(NG - 1, 2, (2, GROUP))
         out_ab(NH - 2, False, True)
         store_part(NG - 1, 2, (2, 3))
         out_c(NG - 1, True, True)

from contextlib import ExitStack

import concourse.mybir as mybir
from concourse.masks import make_identity

BF16 = mybir.dt.bfloat16
F32 = mybir.dt.float32
U32 = mybir.dt.uint32
I32 = mybir.dt.int32
U8 = mybir.dt.uint8
FP8X4 = mybir.dt.float8_e4m3fn_x4
ALU = mybir.AluOpType
ACT = mybir.ActivationFunctionType

B, H, S, D = 8, 4, 512, 128
P = 128
NH = B * H
FLOPS = NH * 2 * (2 * S * S * D)

HEADS = [(2 * pair + i, h) for pair in range(B // 2) for h in range(H) for i in range(2)]
GROUP = 4
VW = D + D // 4
NG = NH // GROUP
NP = NG // 2

BANKS = 4
LAG_T = 3
LAG_V = 6
LAG_X = 1
LAG_Q = 2


def tile_parallelretention_fast3_pa_t_kernel(tc, q_scaled, k, v, omask, out):
    nc = tc.nc
    with ExitStack() as ctx:
        const = ctx.enter_context(tc.tile_pool(name="const", bufs=1))
        res = ctx.enter_context(tc.tile_pool(name="res", bufs=1))
        work = ctx.enter_context(tc.tile_pool(name="work", bufs=3))
        psum = ctx.enter_context(tc.psum_pool(name="psum", bufs=1))

        ctx.enter_context(tc.manual_schedule())
        ident_b = const.tile([P, P], BF16, name="ident_b")
        make_identity(nc, ident_b[:])
        ident_f = const.tile([P, P], F32, name="ident_f")
        make_identity(nc, ident_f[:])

        q_sb, k_sb, v_sb, om_sb, vq = [], [], [], [], []
        for b in range(B):
            q_sb.append(res.tile([P, H * 4, D], BF16, name="q_sb%d" % b))
            k_sb.append(res.tile([P, H * 2, 2 * D], BF16, name="k_sb%d" % b))
            v_sb.append(res.tile([P, H, 4 * D], BF16, name="v_sb%d" % b))
        for p in range(NP):
            vq.append(res.tile([P, 2 * GROUP, VW], U32, name="vq%d" % p, align_bytes=64))
        for h in range(H):
            om_sb.append(res.tile([P, 4, S], BF16, name="om_sb%d" % h))

        ab_tiles, rs_tiles = [], []
        for i in range(3):
            t = res.tile([P, 2, 2, 2 * P], BF16, name="ab_tile%d" % i)
            nc.vector.memset(t[:, 1, :, 192:256], 0.0)
            ab_tiles.append(t)
            t = res.tile([P, 4 * GROUP, 2], F32, name="rs_tile%d" % i)
            nc.vector.memset(t[:], 1.0)
            rs_tiles.append(t)
        vc, vd = [], []
        for i in range(2):
            vc.append(res.tile([P, 2 * GROUP, VW], U32, name="vc%d" % i, align_bytes=64))
            vd.append(res.tile([P, 2 * GROUP, VW], U32, name="vd%d" % i, align_bytes=64))

        def load_k(b, h, nh):
            nc.sync.dma_start(out=k_sb[b][:, 2 * h:2 * (h + nh), :],
                              in_=k[b, h:h + nh].rearrange("h (i r m) d -> r (h i) (m d)", i=2, m=2))

        def load_q(b, h, nh):
            nc.sync.dma_start(out=q_sb[b][:, 4 * h:4 * (h + nh), :],
                              in_=q_scaled[b, h:h + nh].rearrange("h (c r) d -> r (h c) d", r=P))

        def load_v(b, h, nh):
            nc.sync.dma_start(out=v_sb[b][:, h:h + nh, :],
                              in_=v[b, h:h + nh].rearrange("h (p t) d -> p h (t d)", t=4))

        def load_mask(h):
            rows = omask[0, h].rearrange("(c r) j -> r c j", r=P)
            for i in range(2):
                nc.sync.dma_start(out=om_sb[h][:, 2 * i:2 * i + 2, 0:256 * (i + 1)],
                                  in_=rows[:, 2 * i:2 * i + 2, 0:256 * (i + 1)])

        def load_part(p, part):
            b = 2 * p + part % 2
            (load_v, load_k, load_q)[part // 2](b, 0, H)

        qkT, sc_c, sc_d = {}, {}, {}
        gab, gc0, gc1d = {}, {}, {}
        codes, scales, codes0, scales0, codes1, scales1 = {}, {}, {}, {}, {}, {}
        rp, p_max, vg, o_sb, qk_ps, sc_ps, bank_of = {}, {}, {}, {}, {}, {}, {}
        free_banks = list(range(BANKS))

        def t_qk(n, part):
            b, h = HEADS[n]
            if part == 0:
                qk_ps[n] = psum.tile([P, 2 * S], BF16, name="qk_ps")
            for idx in range(4 * part, 4 * part + 4):
                if idx < 4:
                    i, m = divmod(idx, 2)
                    dst = qk_ps[n][:, 256 * m + P * i:256 * m + P * (i + 1)]
                    row = k_sb[b][:, 2 * h + i, m * D:(m + 1) * D]
                else:
                    c = idx - 4
                    dst = qk_ps[n][:, S + P * c:S + P * (c + 1)]
                    row = q_sb[b][:, 4 * h + c, :]
                nc.tensor.transpose(dst, row, ident_b[:])
            if part == 1:
                qkT[n] = work.tile([P, 2 * S], BF16, name="qkT", bufs=4)
                nc.scalar.copy(out=qkT[n][:].bitcast(F32), in_=qk_ps[n][:].bitcast(F32))

        def score_mm(n, chunks):
            bank = free_banks.pop(0)
            s_ps = psum.tile([P, S], F32, name="s_ps%d" % bank)
            for c in chunks:
                half = 64 * (c + 1)
                at = 256 if c == 0 else 0
                sc = s_ps[:, at:at + 2 * half].rearrange("q (u x) -> q u x", u=2)
                nc.tensor.matmul(out=sc, lhsT=qkT[n][:, S + c * P:S + (c + 1) * P],
                                 rhs=qkT[n][:, 0:S].rearrange("d (u x) -> d u x", u=2)[:, :, 0:half],
                                 start=True, stop=True)
                sc_ps[n, c] = sc
            bank_of[n, chunks] = bank

        def score_mask(n, chunks):
            for c in reversed(chunks):
                mask_product(n, c)
            free_banks.append(bank_of[n, chunks])

        def mask_product(n, c):
            g, j = divmod(n, GROUP)
            if g not in sc_c:
                sc_c[g] = work.tile([P, 2, 2, 2 * P], BF16, name="sc_c", bufs=2)
                sc_d[g] = work.tile([P, 2, 2 * P], BF16, name="sc_d", bufs=2)
            h = HEADS[n][1]
            half = 64 * (c + 1)
            if c == 3:
                dst = ab_tiles[n % 3][:, 0, :, :]
            elif c == 2:
                dst = ab_tiles[n % 3][:, 1, :, 0:half]
            elif c == 1:
                dst = sc_c[g][:, j // 2, :, (j % 2) * half:(j % 2 + 1) * half]
            else:
                dst = sc_d[g][:, :, j * half:(j + 1) * half]
            nc.vector.scalar_tensor_tensor(
                out=dst, in0=sc_ps[n, c], scalar=1.0,
                in1=om_sb[h][:, c, 0:2 * half].rearrange("q (x u) -> q u x", u=2),
                op0=ALU.mult, op1=ALU.mult, accum_out=rs_tiles[g % 3][:, 4 * j + c, 0:1])

        def t_slot(bank, slot, nslots, src):
            words = src.rearrange("q u x -> q (u x)").bitcast(F32)
            for u in range(2):
                nc.tensor.transpose(bank[:, (u * nslots + slot) * P:(u * nslots + slot + 1) * P],
                                    words[:, u * P:(u + 1) * P], ident_f[:])

        def x_out(dst, bank, nslots, on_vector=False):
            copy = nc.vector.tensor_copy if on_vector else nc.scalar.copy
            copy(out=dst.bitcast(F32).rearrange("p (x u) -> p x u", u=2),
                 in_=bank[:, 0:nslots * 256].rearrange("p (u x) -> p x u", u=2))

        def t_ab(n):
            x_ab = psum.tile([P, S], F32, name="x_ps", bufs=2)
            for slot in range(2):
                t_slot(x_ab, slot, 2, ab_tiles[n % 3][:, slot, :, :])
            if n % 2 == 0:
                gab[n // 2] = work.tile([P, 4 * S], BF16, name="gab", bufs=2, align_bytes=64)
            x_out(gab[n // 2][:, 2 * S * (n % 2):2 * S * (n % 2 + 1)], x_ab, 2)

        def t_c0(g):
            x_cd = psum.tile([P, S], F32, name="x_ps", bufs=2)
            t_slot(x_cd, 0, 1, sc_c[g][:, 0, :, :])
            gc0[g] = work.tile([P, S], BF16, name="gc0", bufs=2, align_bytes=64)
            x_out(gc0[g][:], x_cd, 1)

        def t_c1d(g):
            x_cd = psum.tile([P, S], F32, name="x_ps", bufs=2)
            t_slot(x_cd, 0, 2, sc_c[g][:, 1, :, :])
            t_slot(x_cd, 1, 2, sc_d[g][:])
            gc1d[g] = work.tile([P, 2 * S], BF16, name="gc1d", bufs=2, align_bytes=64)
            x_out(gc1d[g][:], x_cd, 2, on_vector=g == NG - 1)

        def quant(dst_codes, dst_scales, key, src, width, nm, bufs, halves=(0, 1)):
            if halves[0] == 0:
                dst_codes[key] = work.tile([P, width // 4], U32, name="codes_" + nm, bufs=bufs, align_bytes=64)
                dst_scales[key] = work.tile([P, width // 4], U8, name="scales_" + nm, bufs=bufs, align_bytes=64)
            lo, hi = halves[0] * width // 2, (halves[-1] + 1) * width // 2
            nc.vector.quantize_mx(out=dst_codes[key][:, lo // 4:hi // 4].bitcast(FP8X4),
                                  scales=dst_scales[key][:, lo // 4:hi // 4], in_=src[key][:, lo:hi])

        def v_regroup(n):
            b, h = HEADS[n]
            vg[n] = work.tile([P, D, 4], BF16, name="vg", bufs=2, align_bytes=64)
            nc.gpsimd.tensor_scalar(out=vg[n][:].rearrange("p d (u e) -> p d u e", u=2),
                                    in0=v_sb[b][:, h, :].rearrange("p (e u d) -> p d u e", e=2, u=2),
                                    scalar1=1.0, scalar2=0.0, op0=ALU.mult, op1=ALU.add)

        def v_codes(tiles, n):
            return tiles[:, n % (2 * GROUP), 0:D]

        def v_scales(tiles, n):
            return tiles[:, n % (2 * GROUP), D:VW].bitcast(U8)

        def v_quant(n):
            t = vq[n // (2 * GROUP)]
            nc.vector.quantize_mx(out=v_codes(t, n).bitcast(FP8X4), scales=v_scales(t, n),
                                  in_=vg[n][:].rearrange("p d t -> p (d t)"))

        def v_move(p):
            src = vq[p][:].bitcast(I32)
            c_dst, d_dst = vc[p % 2][:].bitcast(I32), vd[p % 2][:].bitcast(I32)
            for i in range(2):
                nc.sync.dma_start(out=c_dst[64 * i:64 * i + 64, i::2, :], in_=src[0:64, i::2, :])
            for j in range(GROUP):
                nc.sync.dma_start(out=d_dst[32 * j:32 * j + 32, j::GROUP, :], in_=src[0:32, j::GROUP, :])

        def p_ops(g, part, heads=(0, GROUP)):
            cols = slice(4 * heads[0], 4 * heads[1])
            if g not in rp:
                p_max[g] = work.tile([P, 4 * GROUP], F32, name="p_max")
                rp[g] = work.tile([P, 4 * GROUP], F32, name="rp")
            if part == 0:
                nc.vector.tensor_reduce(out=p_max[g][:, cols], in_=rs_tiles[g % 3][:, cols, :], op=ALU.max,
                                        axis=mybir.AxisListType.X, apply_absolute_value=True)
            else:
                nc.vector.reciprocal(out=rp[g][:, cols], in_=p_max[g][:, cols])

        def p_part(step, part):
            g, j = divmod(step, GROUP)
            if j == 0 and 0 < g < NG:
                p_ops(g - 1, part)
            if step == NH - 2:
                p_ops(g, part, (0, 2))

        def mx(o, lc, ls, tiles, n):
            nc.tensor.matmul_mx(out=o, lhsT=lc.bitcast(FP8X4), lhsT_scale=ls,
                                rhs=v_codes(tiles, n).bitcast(FP8X4), rhs_scale=v_scales(tiles, n),
                                start=True, stop=True)

        def scaled(n, c, src, on_vector):
            g, j = divmod(n, GROUP)
            factor = rp[g][:, 4 * j + c:4 * j + c + 1]
            dst = o_sb[g, j % 2][:, j // 2, c, :]
            if on_vector:
                nc.vector.tensor_scalar_mul(out=dst, in0=src, scalar1=factor)
            else:
                nc.scalar.activation(out=dst, in_=src, func=ACT.Copy, scale=factor)

        def out_bank(last_group):
            if last_group:
                k = free_banks.pop(0)
                free_banks.append(k)
                bank = psum.tile([P, S], F32, name="s_ps%d" % k)
            else:
                bank = psum.tile([P, S], F32, name="o_ps")
            return bank

        def out_ab(n0, on_vector, last_group=False):
            g = n0 // GROUP
            o_ps = out_bank(last_group)
            parts = [(n0 + i // 2, 3 - i % 2) for i in range(4)]
            for i, (n, c) in enumerate(parts):
                slot = slice(i * P, (i + 1) * P)
                mx(o_ps[:, slot], codes[n // 2][:, slot], scales[n // 2][:, slot], vq[g // 2], n)
            if n0 % GROUP == 0:
                for i in range(2):
                    o_sb[g, i] = work.tile([P, 2, 4, D], F32, name="o_sb", bufs=4)
            for i, (n, c) in enumerate(parts):
                scaled(n, c, o_ps[:, i * P:(i + 1) * P], on_vector)

        def out_c(g, on_vector, last_group=False):
            o_ps = out_bank(last_group)
            for j in range(GROUP):
                lc, ls = ((codes0[g], scales0[g]), (codes1[g], scales1[g]))[j // 2]
                mx(o_ps[:, j * P:(j + 1) * P], lc[:, 0:P], ls[:, 0:P], vc[g // 2 % 2], GROUP * g + j)
            for j in range(GROUP):
                scaled(GROUP * g + j, 1, o_ps[:, j * P:(j + 1) * P], on_vector)

        def out_d(g, on_vector, last_group=False):
            o_ps = out_bank(last_group)
            for j in range(GROUP):
                mx(o_ps[:, j * P:(j + 1) * P], codes1[g][:, P:2 * P], scales1[g][:, P:2 * P],
                   vd[g // 2 % 2], GROUP * g + j)
            for j in range(GROUP):
                scaled(GROUP * g + j, 0, o_ps[:, j * P:(j + 1) * P], on_vector)

        def store(g):
            b, h = HEADS[GROUP * g]
            for i in range(2):
                nc.sync.dma_start(out=out[b + i, h:h + 2].rearrange("h (c r) d -> r (h c) d", r=P),
                                  in_=o_sb[g, i][:].rearrange("p h c d -> p (h c) d"))

        def store_chunk(g, c):
            b, h = HEADS[GROUP * g]
            for i in range(2):
                nc.sync.dma_start(out=out[b + i, h:h + 2].rearrange("h (c r) d -> r h c d", r=P)[:, :, c, :],
                                  in_=o_sb[g, i][:, :, c, :])

        def store_part(g, c0, heads=range(GROUP)):
            for j in heads:
                b, h = HEADS[GROUP * g + j]
                nc.sync.dma_start(out=out[b, h].rearrange("(c r) d -> r c d", r=P)[:, c0:c0 + 2, :],
                                  in_=o_sb[g, j % 2][:, j // 2, c0:c0 + 2, :])

        for h in range(H):
            for b in range(2):
                load_k(b, h, 1)
                load_q(b, h, 1)
                if b == 0 and h < 2:
                    load_mask(h)
            for b in range(2):
                load_v(b, h, 1)
            if h >= 2:
                load_mask(h)
        for b in (2, 3):
            load_v(b, 0, H)
        for b in (2, 3):
            load_k(b, 0, 2)
            load_q(b, 0, 2)
        for t in vq:
            nc.vector.memset(t[:, :, D:VW].bitcast(I32), 0)
        for t in vc + vd:
            nc.vector.memset(t[:].bitcast(I32), 0)
        for part in range(2):
            t_qk(0, part)
        for chunks in ((0, 1), (2,), (3,)):
            score_mm(0, chunks)
        for part in range(2):
            t_qk(1, part)
        for n in range(6):
            v_regroup(n)

        for step in range(NH + 1):
            g, j = divmod(step, GROUP)
            live, ahead = step < NH, step + 1 < NH
            order = ((0, 1), (2,), (3,)) if step == 0 else ((3,), (2,), (0, 1))
            p_part(step, 0)
            if live:
                score_mask(step, order[0])
            if j == 0 and g > 1 and live:
                out_d(g - 2, False)
            elif j == 1 and g > 0:
                out_ab(step - 5, False)
                if g > 1:
                    store(g - 2)
            elif j == 2 and g > 0:
                out_ab(step - 4, False)
                if g == NG - 1:
                    store_part(g - 1, 2)
            elif j == 3 and g > 0:
                out_c(g - 1, False)
            last = step - LAG_X
            if 0 <= last < NH - 1:
                t_ab(last)
            if 0 <= last < NH - 1 and last % GROUP == 1:
                t_c0(last // GROUP)
            if 0 <= last < NH - 1 and last % GROUP == 3:
                t_c1d(last // GROUP)
            if step == 2:
                for part in range(2):
                    t_qk(step + LAG_T - 1, part)
            if ahead:
                score_mm(step + 1, (0, 1))
                score_mm(step + 1, (2,))
            if live:
                score_mask(step, order[1])
            if ahead:
                score_mm(step + 1, (3,))
            p_part(step, 1)
            m = step - LAG_Q
            if 0 <= m < NH:
                if m % GROUP == 1:
                    quant(codes0, scales0, m // GROUP, gc0, S, "c0", 2)
                if m % GROUP == 3:
                    quant(codes1, scales1, m // GROUP, gc1d, 2 * S, "c1d", 2)
                if m == NH - 2:
                    quant(codes, scales, m // 2, gab, 4 * S, "ab", 3, (0,))
                elif m % 2 == 1:
                    quant(codes, scales, m // 2, gab, 4 * S, "ab", 3)
            n = step + (LAG_T if step >= 2 else LAG_T - 1)
            if n < NH:
                for part in range(2):
                    t_qk(n, part)
            if live:
                score_mask(step, order[2])
            if step == NH - 1:
                t_ab(step)
                out_d(g - 1, False)
                store_part(g - 1, 0)
                out_ab(NH - 4, False, True)
                store_part(g, 2, (0, 1))
            if step == NH:
                t_c1d(g - 1)
            if step + LAG_V < NH:
                v_regroup(step + LAG_V)
            for n in range(NH):
                if step == (n // 2 + 1 if n < 2 * GROUP else n - 3):
                    v_quant(n)
                    if n % (2 * GROUP) == 2 * GROUP - 1:
                        v_move(n // (2 * GROUP))
            if step == 4:
                for b in (2, 3):
                    load_k(b, 2, 2)
                    load_q(b, 2, 2)
            pair, part = divmod(step - 5, 8)
            if step >= 5 and part < 6 and pair + 2 < NP:
                load_part(pair + 2, part)
        p_ops(NG - 1, 0, (2, GROUP))
        quant(codes, scales, NH // 2 - 1, gab, 4 * S, "ab", 3, (1,))
        p_ops(NG - 1, 1, (2, GROUP))
        quant(codes1, scales1, NG - 1, gc1d, 2 * S, "c1d", 2)
        out_ab(NH - 2, False, True)
        store_part(NG - 1, 2, (2, 3))
        out_c(NG - 1, True, True)
        store_chunk(NG - 1, 1)
        out_d(NG - 1, True, True)
        store_chunk(NG - 1, 0)
